import numpy as np
import ml_dtypes


def mxq(x, axis, fmt="e4m3"):
    dtype, down = {"e4m3": (ml_dtypes.float8_e4m3fn, 7), "e5m2": (ml_dtypes.float8_e5m2, 14)}[fmt]
    v = np.moveaxis(np.asarray(x, np.float32).astype(ml_dtypes.bfloat16).astype(np.float64), axis, -1)
    blocks = v.reshape(v.shape[:-1] + (-1, 32))
    amax = np.abs(blocks).max(-1, keepdims=True)
    byte = np.maximum(np.where(amax > 0, np.frexp(amax)[1] - 1 + 127, 0) - down, 1)
    scale = np.exp2(byte - 127.0)
    codes = (blocks / scale).astype(np.float32).astype(dtype).astype(np.float64)
    return np.moveaxis((codes * scale).reshape(v.shape), -1, axis)


WIDE = False


def mx_kscale(k):
    if not WIDE:
        return np.ones(k)
    levels = np.array([10, -10, 5, -5, 0])
    if k % 512:
        return np.exp2(np.random.permutation(np.resize(levels, k // 32))).repeat(32)
    a = np.empty((k // 512, 16))
    for p in range(k // 512):
        a[p, :8] = np.random.permutation(np.resize(levels, 8))
        for g in range(8):
            far = levels[np.abs(levels - a[p, g]) >= 10]
            a[p, g + 8] = far[np.random.randint(len(far))]
    return np.exp2(a.ravel()).repeat(32)


BF16 = ml_dtypes.bfloat16


def bf(x):
    return np.asarray(x, np.float32).astype(BF16)


def f64(x):
    return np.asarray(x).astype(np.float64)


B, N, D, F = 4, 32, 512, 512


def setup_inputs():
    s, t = mx_kscale(D), mx_kscale(D)
    ss = np.concatenate([s, s])
    sst = np.concatenate([s, s, t])
    return {
        'text_embedding': bf(np.random.standard_normal((B, N, D)) * s),
        'W_rel': bf(np.random.standard_normal((2 * D, D)) / np.sqrt(2 * D) / ss[:, None] * t),
        'b_rel': bf(np.random.standard_normal(D) * 0.3 * t),
        'W_go': bf(np.random.standard_normal((D, D)) / np.sqrt(D) / s[:, None]),
        'b_go': bf(np.random.standard_normal(D) * 0.3),
        'W_gr': bf(np.random.standard_normal((3 * D, F)) * 1.5 / np.sqrt(3 * D) / sst[:, None]),
        'b_gr': bf(np.random.standard_normal(F) * 0.3),
    }


def reference(text_embedding, W_rel, b_rel, W_go, b_go, W_gr, b_gr):
    xq = mxq(f64(text_embedding), 2, 'e4m3')
    wr, wg = f64(W_rel), f64(W_gr)
    new_x = np.tanh((xq @ mxq(f64(W_go), 0, 'e4m3')) + f64(b_go))
    rel0 = ((xq @ mxq(wr[:D], 0, 'e4m3'))[:, :, None, :]
            + (xq @ mxq(wr[D:], 0, 'e4m3'))[:, None, :, :] + f64(b_rel))
    pre = ((xq @ mxq(wg[:D], 0, 'e4m3'))[:, :, None, :]
           + (xq @ mxq(wg[D:2 * D], 0, 'e4m3'))[:, None, :, :]
           + (mxq(rel0, 3, 'e4m3') @ mxq(wg[2 * D:], 0, 'e4m3')) + f64(b_gr))
    return new_x, np.tanh(pre)

@@ -1,0 +1,324 @@
+from contextlib import ExitStack
+
+import concourse.mybir as mybir
+from concourse.masks import make_identity
+
+BF16 = mybir.dt.bfloat16
+F32 = mybir.dt.float32
+I32 = mybir.dt.int32
+U32 = mybir.dt.uint32
+U8 = mybir.dt.uint8
+FP8X4 = mybir.dt.float8_e4m3fn_x4
+ADD = mybir.AluOpType.add
+TANH = mybir.ActivationFunctionType.Tanh
+
+P = 128
+PACK = 4
+BATCH = 4
+NODES = 32
+TOKENS = BATCH * NODES
+D = P * PACK
+F = 512
+PAIRS = BATCH * NODES * NODES
+I_PER_TILE = P // NODES
+I_PER_CHUNK = 16
+COLS_PER_CHUNK = I_PER_CHUNK * NODES
+TILES_PER_CHUNK = COLS_PER_CHUNK // P
+CHUNKS = PAIRS // COLS_PER_CHUNK
+CHUNKS_PER_BATCH = NODES // I_PER_CHUNK
+BYTES_PER_WORD = 4
+GPSIMD_I = 10
+
+BY_FEATURE = "(p t) n -> p t n"
+
+FLOPS = 2 * (5 * TOKENS * D * F + PAIRS * D * F)
+
+
+def load_weight(nc, pool, rows, name):
+    raw = pool.tile([P, PACK, F], BF16, name=name)
+    nc.sync.dma_start(out=raw[:], in_=rows.rearrange(BY_FEATURE, p=P))
+    return raw
+
+
+def regroup_weight(pool, copy, raw, name):
+    grouped = pool.tile([P, F, PACK], BF16, name=name, align_bytes=64)
+    copy(
+        out=grouped[:].rearrange("p (c i) t -> p c t i", i=4),
+        in_=raw[:].rearrange("p t (c i) -> p c t i", i=4),
+    )
+    return grouped
+
+
+def regroup_by_channel(pool, copy, raw, name):
+    grouped = pool.tile([P, F, PACK], BF16, name=name, align_bytes=64)
+    copy(
+        out=grouped[:].rearrange("p (t m) j -> p t m j", t=PACK),
+        in_=raw[:].rearrange("p j (m t) -> p t m j", t=PACK),
+    )
+    return grouped
+
+
+def quantise_weight(nc, pool, grouped, name):
+    codes = pool.tile([P, F], U32, name=name + "_codes", align_bytes=64)
+    scales = pool.tile([P, F], U8, name=name + "_scales", align_bytes=64)
+    nc.vector.quantize_mx(
+        out=codes[:].bitcast(FP8X4), scales=scales[:], in_=grouped[:].rearrange("p n t -> p (n t)")
+    )
+    return codes, scales
+
+
+def columns(operand, first, count):
+    codes, scales = operand
+    return codes[:, first : first + count], scales[:, first : first + count]
+
+
+def mx_pass(nc, out, stationary, moving, start, stop):
+    nc.tensor.matmul_mx(
+        out=out,
+        lhsT=stationary[0].bitcast(FP8X4),
+        lhsT_scale=stationary[1],
+        rhs=moving[0].bitcast(FP8X4),
+        rhs_scale=moving[1],
+        start=start,
+        stop=stop,
+    )
+
+
+def tile_languagemsgencoder_pa_kernel(
+    tc, text_embedding, W_rel, b_rel, W_go, b_go, W_gr, b_gr, out_0, out_1
+):
+    nc = tc.nc
+    new_x_rows = out_0.rearrange("b n f -> (b n) f")
+    rel_rows = out_1.rearrange("b i j f -> (b i j) f")
+
+    with ExitStack() as ctx:
+        keep = ctx.enter_context(tc.tile_pool(name="keep", bufs=1))
+        stream = ctx.enter_context(tc.tile_pool(name="stream", bufs=1))
+        results = ctx.enter_context(tc.tile_pool(name="results", bufs=8))
+        keep_ps = ctx.enter_context(tc.psum_pool(name="keep_ps", bufs=1))
+        setup_ps = ctx.enter_context(tc.psum_pool(name="setup_ps", bufs=3))
+        acc_ps = ctx.enter_context(tc.psum_pool(name="acc_ps", bufs=TILES_PER_CHUNK))
+        ctx.enter_context(tc.manual_schedule())
+
+        x_sb = keep.tile([P, D], BF16)
+        nc.sync.dma_start(out=x_sb[:], in_=text_embedding.rearrange("b n d -> (b n) d"))
+        rb_raw = load_weight(nc, keep, W_rel[D : 2 * D, :], "rb_raw")
+        ra_raw = load_weight(nc, keep, W_rel[0:D, :], "ra_raw")
+        ga_raw = load_weight(nc, keep, W_gr[0:D, :], "ga_raw")
+        gb_raw = load_weight(nc, keep, W_gr[D : 2 * D, :], "gb_raw")
+        gc_raw = load_weight(nc, keep, W_gr[2 * D : 3 * D, :], "gc_raw")
+        go_raw = load_weight(nc, keep, W_go, "go_raw")
+
+        bias_rows = keep.tile([P, 3, F], BF16)
+        nc.vector.memset(bias_rows[:], 0.0)
+        nc.scalar.dma_start(out=bias_rows[0:1, 2, :], in_=b_rel.rearrange("(o f) -> o f", o=1))
+        nc.scalar.dma_start(out=bias_rows[0:1, 0, :], in_=b_gr.rearrange("(o f) -> o f", o=1))
+        nc.scalar.dma_start(out=bias_rows[0:1, 1, :], in_=b_go.rearrange("(o f) -> o f", o=1))
+
+        warm = keep.tile([P, 1], F32)
+        nc.vector.memset(warm[:], 0.0)
+        nc.scalar.activation(out=warm[:], in_=warm[:], func=TANH)
+
+        ident = keep.tile([P, P], F32)
+        make_identity(nc, ident[:])
+        ones = keep.tile([P, P], BF16)
+        nc.vector.memset(ones[:], 1.0)
+
+        x_codes = keep.tile([P, TOKENS], U32, align_bytes=64)
+        x_scales = keep.tile([P, TOKENS], U8, align_bytes=64)
+        x4_codes = keep.tile([P, TOKENS * BYTES_PER_WORD], U32, align_bytes=64)
+        x4_scales = keep.tile([P, TOKENS * BYTES_PER_WORD], U8, align_bytes=64)
+        nc.vector.memset(x_scales[:].bitcast(I32), 0)
+        nc.vector.memset(x4_scales[:].bitcast(I32), 0)
+
+        x_words = x_sb[:].bitcast(F32)
+        x_t = setup_ps.tile([P, 2, TOKENS], F32, tag="setup")
+        for u in range(2):
+            nc.tensor.transpose(x_t[:, u, :], x_words[:, u : D // 2 : 2], ident[:])
+        x_grouped = keep.tile([P, TOKENS, PACK], BF16, align_bytes=64)
+        nc.scalar.copy(
+            out=x_grouped[:].rearrange("p r t -> p (r t)").bitcast(F32).rearrange("p (r u) -> p r u", u=2),
+            in_=x_t[:].rearrange("p u r -> p r u"),
+        )
+        x_fourfold = keep.tile([P, TOKENS, BYTES_PER_WORD, PACK], BF16, align_bytes=64)
+        nc.vector.tensor_copy(
+            out=x_fourfold[:],
+            in_=x_grouped[:].unsqueeze(2).to_broadcast([P, TOKENS, BYTES_PER_WORD, PACK]),
+        )
+        nc.vector.quantize_mx(
+            out=x_codes[:].bitcast(FP8X4), scales=x_scales[:], in_=x_grouped[:].rearrange("p r t -> p (r t)")
+        )
+        x_mx = (x_codes[:], x_scales[:])
+
+        brel_t = setup_ps.tile([P, PACK], F32, tag="setup")
+        for t in range(PACK):
+            nc.tensor.matmul(
+                out=brel_t[:, t : t + 1], lhsT=bias_rows[:, 2, t:F:PACK], rhs=ones[:, 0:1], start=True, stop=True
+            )
+        bgr_ps = setup_ps.tile([P, F], F32, tag="setup")
+        nc.tensor.matmul(out=bgr_ps[:], lhsT=ones[:], rhs=bias_rows[:, 0, :], start=True, stop=True)
+        bgo_ps = setup_ps.tile([P, F], F32, tag="setup")
+        nc.tensor.matmul(out=bgo_ps[:], lhsT=ones[:], rhs=bias_rows[:, 1, :], start=True, stop=True)
+
+        rb_grouped = regroup_by_channel(keep, nc.scalar.copy, rb_raw, "rb_grouped")
+
+        xj_codes = keep.tile([P, TOKENS * I_PER_TILE], U32, align_bytes=64)
+        xj_scales = keep.tile([P, TOKENS * I_PER_TILE], U8, align_bytes=64)
+        nc.vector.tensor_copy(
+            out=xj_codes[:].bitcast(I32).rearrange("p (b c j) -> p b c j", b=BATCH, c=I_PER_TILE),
+            in_=x_codes[:]
+            .bitcast(I32)
+            .rearrange("p (b j) -> p b j", b=BATCH)
+            .unsqueeze(2)
+            .to_broadcast([P, BATCH, I_PER_TILE, NODES]),
+        )
+        nc.vector.tensor_copy(
+            out=xj_scales[:].bitcast(I32).rearrange("p (b c w) -> p b c w", b=BATCH, c=I_PER_TILE),
+            in_=x_scales[:]
+            .bitcast(I32)
+            .rearrange("p (b w) -> p b w", b=BATCH)
+            .unsqueeze(2)
+            .to_broadcast([P, BATCH, I_PER_TILE, NODES // BYTES_PER_WORD]),
+        )
+        xj = (xj_codes, xj_scales)
+        nc.vector.quantize_mx(
+            out=x4_codes[:].bitcast(FP8X4),
+            scales=x4_scales[:],
+            in_=x_fourfold[:].rearrange("p r c t -> p (r c t)"),
+        )
+        brel = keep.tile([P, PACK], F32)
+        nc.vector.tensor_copy(out=brel[:], in_=brel_t[:])
+
+        xi_codes = keep.tile([P, PAIRS], U32, align_bytes=64)
+        xi_scales = keep.tile([P, PAIRS], U8, align_bytes=64)
+        xi = (xi_codes, xi_scales)
+        repeats = NODES // BYTES_PER_WORD
+
+        def repeat_xi(b):
+            tokens = slice(b * NODES, (b + 1) * NODES)
+            nc.vector.tensor_copy(
+                out=xi_codes[:]
+                .bitcast(I32)
+                .rearrange("p (r e c) -> p r e c", e=repeats, c=BYTES_PER_WORD)[:, tokens, :, :],
+                in_=x4_codes[:]
+                .bitcast(I32)
+                .rearrange("p (r c) -> p r c", c=BYTES_PER_WORD)[:, tokens, :]
+                .unsqueeze(2)
+                .to_broadcast([P, NODES, repeats, BYTES_PER_WORD]),
+            )
+            nc.vector.tensor_copy(
+                out=xi_scales[:].bitcast(I32).rearrange("p (r e) -> p r e", e=repeats)[:, tokens, :],
+                in_=x4_scales[:].bitcast(I32)[:, tokens].unsqueeze(2).to_broadcast([P, NODES, repeats]),
+            )
+
+        ra_grouped = regroup_by_channel(keep, nc.vector.tensor_copy, ra_raw, "ra_grouped")
+        rb = quantise_weight(nc, keep, rb_grouped, "rb")
+        b_t = setup_ps.tile([P, PACK, TOKENS], F32, tag="setup")
+        for t in range(PACK):
+            mx_pass(nc, b_t[:, t, :], columns(rb, t * P, P), x_mx, start=True, stop=True)
+        ra = quantise_weight(nc, keep, ra_grouped, "ra")
+        a_t = keep_ps.tile([P, PACK, TOKENS], F32)
+        for t in range(PACK):
+            mx_pass(nc, a_t[:, t, :], columns(ra, t * P, P), x_mx, start=True, stop=True)
+        repeat_xi(0)
+        b_plus = keep.tile([P, TOKENS, PACK], F32)
+        nc.vector.tensor_tensor(
+            out=b_plus[:],
+            in0=b_t[:].rearrange("p t r -> p r t"),
+            in1=brel[:].unsqueeze(1).to_broadcast([P, TOKENS, PACK]),
+            op=ADD,
+        )
+        a_sb = keep.tile([P, TOKENS, PACK], F32)
+        nc.vector.tensor_copy(out=a_sb[:], in_=a_t[:].rearrange("p t r -> p r t"))
+        ga_grouped = regroup_weight(keep, nc.scalar.copy, ga_raw, "ga_grouped")
+        gb_grouped = regroup_weight(keep, nc.scalar.copy, gb_raw, "gb_grouped")
+        gc_grouped = regroup_weight(keep, nc.scalar.copy, gc_raw, "gc_grouped")
+        bgr = keep.tile([P, F], F32)
+        nc.scalar.copy(out=bgr[:], in_=bgr_ps[:])
+        go_grouped = regroup_weight(keep, nc.scalar.copy, go_raw, "go_grouped")
+        bgo = keep.tile([P, F], F32)
+        nc.scalar.copy(out=bgo[:], in_=bgo_ps[:])
+
+        rel0_codes = keep.tile([P, PAIRS], U32, align_bytes=64)
+        rel0_scales = keep.tile([P, PAIRS], U8, align_bytes=64)
+        rel0_mx = (rel0_codes, rel0_scales)
+
+        def form_rel0(chunk, gpsimd_i):
+            first_token = chunk * I_PER_CHUNK
+            b = first_token // NODES
+            rel0 = stream.tile([P, I_PER_CHUNK, NODES, PACK], BF16, align_bytes=64)
+            b_part = b_plus[:, b * NODES : (b + 1) * NODES, :].unsqueeze(1)
+            nc.gpsimd.tensor_tensor(
+                out=rel0[:, 0:gpsimd_i, :, :],
+                in0=a_sb[:, first_token : first_token + gpsimd_i, :]
+                .unsqueeze(2)
+                .to_broadcast([P, gpsimd_i, NODES, PACK]),
+                in1=b_part.to_broadcast([P, gpsimd_i, NODES, PACK]),
+                op=ADD,
+            )
+            vector_i = I_PER_CHUNK - gpsimd_i
+            nc.vector.tensor_tensor(
+                out=rel0[:, gpsimd_i:I_PER_CHUNK, :, :],
+                in0=a_t[:, :, first_token + gpsimd_i : first_token + I_PER_CHUNK]
+                .rearrange("p t i -> p i t")
+                .unsqueeze(2)
+                .to_broadcast([P, vector_i, NODES, PACK]),
+                in1=b_part.to_broadcast([P, vector_i, NODES, PACK]),
+                op=ADD,
+            )
+            return rel0
+
+        def quantise_rel0(chunk, rel0):
+            chunk_codes, chunk_scales = columns(rel0_mx, chunk * COLS_PER_CHUNK, COLS_PER_CHUNK)
+            nc.vector.quantize_mx(
+                out=chunk_codes.bitcast(FP8X4), scales=chunk_scales, in_=rel0[:].rearrange("p i j t -> p (i j t)")
+            )
+
+        def open_tile(first_row):
+            b = first_row // (NODES * NODES)
+            acc = acc_ps.tile([P, F], F32)
+            mx_pass(nc, acc[:], columns(xi, first_row, P), columns(ga, 0, F), start=True, stop=False)
+            mx_pass(nc, acc[:], columns(xj, b * P, P), columns(gb, 0, F), start=False, stop=False)
+            return acc
+
+        def close_tile(acc, first_row):
+            mx_pass(nc, acc[:], columns(rel0_mx, first_row, P), columns(gc, 0, F), start=False, stop=True)
+
+        def finish(acc, bias, rows):
+            result = results.tile([P, F], F32)
+            nc.vector.tensor_tensor(out=result[:], in0=acc[:], in1=bias[:], op=ADD)
+            nc.scalar.activation(out=result[:], in_=result[:], func=TANH)
+            nc.sync.dma_start(out=rows, in_=result[:])
+
+        def first_row_of(chunk, n):
+            return chunk * COLS_PER_CHUNK + n * P
+
+        def finish_rel(chunk, n, acc):
+            finish(acc, bgr, rel_rows[first_row_of(chunk, n) : first_row_of(chunk, n) + P, :])
+
+        rel0 = form_rel0(0, I_PER_CHUNK - GPSIMD_I)
+        ga = quantise_weight(nc, keep, ga_grouped, "ga")
+        gb = quantise_weight(nc, keep, gb_grouped, "gb")
+        accs = [open_tile(first_row_of(0, n)) for n in range(TILES_PER_CHUNK)]
+        gc = quantise_weight(nc, keep, gc_grouped, "gc")
+        quantise_rel0(0, rel0)
+        for n in range(TILES_PER_CHUNK):
+            close_tile(accs[n], first_row_of(0, n))
+
+        for chunk in range(1, CHUNKS):
+            rel0 = form_rel0(chunk, GPSIMD_I)
+            for n in range(TILES_PER_CHUNK):
+                finish_rel(chunk - 1, n, accs[n])
+                accs[n] = open_tile(first_row_of(chunk, n))
+            if (chunk + 1) % CHUNKS_PER_BATCH == 0 and chunk + 1 < CHUNKS:
+                repeat_xi((chunk + 1) // CHUNKS_PER_BATCH)
+            quantise_rel0(chunk, rel0)
+            for n in range(TILES_PER_CHUNK):
+                close_tile(accs[n], first_row_of(chunk, n))
+
+        go = quantise_weight(nc, keep, go_grouped, "go")
+        new_x_acc = setup_ps.tile([P, F], F32, tag="setup")
+        mx_pass(nc, new_x_acc[:], x_mx, columns(go, 0, F), start=True, stop=True)
+        for n in range(TILES_PER_CHUNK):
+            finish_rel(CHUNKS - 1, n, accs[n])
+        finish(new_x_acc, bgo, new_x_rows)

@@ -20,42 +20,38 @@ TOKENS = BATCH * NODES
 D = P * PACK
 F = 512
 PAIRS = BATCH * NODES * NODES
-I_PER_TILE = P // NODES
-I_PER_CHUNK = 16
-COLS_PER_CHUNK = I_PER_CHUNK * NODES
-TILES_PER_CHUNK = COLS_PER_CHUNK // P
-CHUNKS = PAIRS // COLS_PER_CHUNK
-CHUNKS_PER_BATCH = NODES // I_PER_CHUNK
-BYTES_PER_WORD = 4
-GPSIMD_I = 10
+HALF = F // 2
 
-BY_FEATURE = "(p t) n -> p t n"
+CHUNKS = [2, 4, 4, 4, 4, 4, 4, 4, 2]
+MAX_CHUNK = max(CHUNKS)
+GPSIMD_I = 20
+
 
 FLOPS = 2 * (5 * TOKENS * D * F + PAIRS * D * F)
 
 
 def load_weight(nc, pool, rows, name):
     raw = pool.tile([P, PACK, F], BF16, name=name)
-    nc.sync.dma_start(out=raw[:], in_=rows.rearrange(BY_FEATURE, p=P))
+    nc.sync.dma_start(out=raw[:], in_=rows.rearrange("(p t) n -> p t n", p=P))
     return raw
 
 
-def regroup_weight(pool, copy, raw, name):
-    grouped = pool.tile([P, F, PACK], BF16, name=name, align_bytes=64)
-    copy(
-        out=grouped[:].rearrange("p (c i) t -> p c t i", i=4),
-        in_=raw[:].rearrange("p t (c i) -> p c t i", i=4),
-    )
-    return grouped
+def new_grouped(pool, name):
+    return pool.tile([P, F, PACK], BF16, name=name, align_bytes=64)
 
 
-def regroup_by_channel(pool, copy, raw, name):
-    grouped = pool.tile([P, F, PACK], BF16, name=name, align_bytes=64)
+def regroup(copy, grouped, raw, first=0, last=F):
     copy(
-        out=grouped[:].rearrange("p (t m) j -> p t m j", t=PACK),
-        in_=raw[:].rearrange("p j (m t) -> p t m j", t=PACK),
+        out=grouped[:, first:last, :].rearrange("p (c i) t -> p c t i", i=4),
+        in_=raw[:, :, first:last].rearrange("p t (c i) -> p c t i", i=4),
     )
-    return grouped
+
+
+def regroup_by_channel(copy, grouped, raw, first, last):
+    copy(
+        out=grouped[:].rearrange("p (t m) j -> p t m j", t=PACK)[:, first:last, :, :],
+        in_=raw[:].rearrange("p j (m t) -> p t m j", t=PACK)[:, first:last, :, :],
+    )
 
 
 def quantise_weight(nc, pool, grouped, name):
@@ -88,32 +84,15 @@ def tile_languagemsgencoder_pa_kernel(
     tc, text_embedding, W_rel, b_rel, W_go, b_go, W_gr, b_gr, out_0, out_1
 ):
     nc = tc.nc
-    new_x_rows = out_0.rearrange("b n f -> (b n) f")
-    rel_rows = out_1.rearrange("b i j f -> (b i j) f")
 
     with ExitStack() as ctx:
         keep = ctx.enter_context(tc.tile_pool(name="keep", bufs=1))
         stream = ctx.enter_context(tc.tile_pool(name="stream", bufs=1))
-        results = ctx.enter_context(tc.tile_pool(name="results", bufs=8))
+        results = ctx.enter_context(tc.tile_pool(name="results", bufs=3))
         keep_ps = ctx.enter_context(tc.psum_pool(name="keep_ps", bufs=1))
         setup_ps = ctx.enter_context(tc.psum_pool(name="setup_ps", bufs=3))
-        acc_ps = ctx.enter_context(tc.psum_pool(name="acc_ps", bufs=TILES_PER_CHUNK))
+        acc_ps = ctx.enter_context(tc.psum_pool(name="acc_ps", bufs=4))
         ctx.enter_context(tc.manual_schedule())
-
-        x_sb = keep.tile([P, D], BF16)
-        nc.sync.dma_start(out=x_sb[:], in_=text_embedding.rearrange("b n d -> (b n) d"))
-        rb_raw = load_weight(nc, keep, W_rel[D : 2 * D, :], "rb_raw")
-        ra_raw = load_weight(nc, keep, W_rel[0:D, :], "ra_raw")
-        ga_raw = load_weight(nc, keep, W_gr[0:D, :], "ga_raw")
-        gb_raw = load_weight(nc, keep, W_gr[D : 2 * D, :], "gb_raw")
-        gc_raw = load_weight(nc, keep, W_gr[2 * D : 3 * D, :], "gc_raw")
-        go_raw = load_weight(nc, keep, W_go, "go_raw")
-
-        bias_rows = keep.tile([P, 3, F], BF16)
-        nc.vector.memset(bias_rows[:], 0.0)
-        nc.scalar.dma_start(out=bias_rows[0:1, 2, :], in_=b_rel.rearrange("(o f) -> o f", o=1))
-        nc.scalar.dma_start(out=bias_rows[0:1, 0, :], in_=b_gr.rearrange("(o f) -> o f", o=1))
-        nc.scalar.dma_start(out=bias_rows[0:1, 1, :], in_=b_go.rearrange("(o f) -> o f", o=1))
 
         warm = keep.tile([P, 1], F32)
         nc.vector.memset(warm[:], 0.0)
@@ -121,106 +100,85 @@ def tile_languagemsgencoder_pa_kernel(
 
         ident = keep.tile([P, P], F32)
         make_identity(nc, ident[:])
+
+        bias_rows = keep.tile([P, 3, F], BF16)
+        nc.vector.memset(bias_rows[:].rearrange("p a f -> p (a f)").bitcast(I32), 0)
         ones = keep.tile([P, P], BF16)
         nc.vector.memset(ones[:], 1.0)
+        ident_bf = keep.tile([P, P], BF16)
+        nc.vector.tensor_copy(out=ident_bf[:], in_=ident[:])
+
+        x_sb = keep.tile([P, D], BF16)
+        for b in range(BATCH):
+            nc.sync.dma_start(out=x_sb[b:P:BATCH, :], in_=text_embedding[b])
+        rb_raw = load_weight(nc, keep, W_rel[D : 2 * D, :], "rb_raw")
+        for row, bias in enumerate((b_rel, b_gr, b_go)):
+            nc.sync.dma_start(out=bias_rows[0:1, row, :], in_=bias.rearrange("(o f) -> o f", o=1))
+        ra_raw = load_weight(nc, keep, W_rel[0:D, :], "ra_raw")
+        gc_raw = load_weight(nc, keep, W_gr[2 * D : 3 * D, :], "gc_raw")
+        gb_raw = load_weight(nc, keep, W_gr[D : 2 * D, :], "gb_raw")
+        ga_raw = load_weight(nc, keep, W_gr[0:D, :], "ga_raw")
+        go_raw = load_weight(nc, keep, W_go, "go_raw")
 
         x_codes = keep.tile([P, TOKENS], U32, align_bytes=64)
         x_scales = keep.tile([P, TOKENS], U8, align_bytes=64)
-        x4_codes = keep.tile([P, TOKENS * BYTES_PER_WORD], U32, align_bytes=64)
-        x4_scales = keep.tile([P, TOKENS * BYTES_PER_WORD], U8, align_bytes=64)
         nc.vector.memset(x_scales[:].bitcast(I32), 0)
-        nc.vector.memset(x4_scales[:].bitcast(I32), 0)
 
         x_words = x_sb[:].bitcast(F32)
         x_t = setup_ps.tile([P, 2, TOKENS], F32, tag="setup")
         for u in range(2):
             nc.tensor.transpose(x_t[:, u, :], x_words[:, u : D // 2 : 2], ident[:])
+        rb_grouped = new_grouped(keep, "rb_grouped")
+        ra_grouped = new_grouped(keep, "ra_grouped")
+        regroup_by_channel(nc.vector.tensor_copy, rb_grouped, rb_raw, 0, 2)
+        regroup_by_channel(nc.scalar.copy, rb_grouped, rb_raw, 2, 4)
         x_grouped = keep.tile([P, TOKENS, PACK], BF16, align_bytes=64)
-        nc.scalar.copy(
+        nc.vector.tensor_copy(
             out=x_grouped[:].rearrange("p r t -> p (r t)").bitcast(F32).rearrange("p (r u) -> p r u", u=2),
             in_=x_t[:].rearrange("p u r -> p r u"),
         )
-        x_fourfold = keep.tile([P, TOKENS, BYTES_PER_WORD, PACK], BF16, align_bytes=64)
-        nc.vector.tensor_copy(
-            out=x_fourfold[:],
-            in_=x_grouped[:].unsqueeze(2).to_broadcast([P, TOKENS, BYTES_PER_WORD, PACK]),
-        )
+        brel_t = setup_ps.tile([P, PACK], F32, tag="setup")
+        for t in range(PACK):
+            nc.tensor.matmul(
+                out=brel_t[:, t : t + 1], lhsT=bias_rows[:, 0, t:F:PACK], rhs=ones[:, 0:1], start=True, stop=True
+            )
+        bgr_ps = setup_ps.tile([P, F], F32, tag="setup")
+        nc.tensor.matmul(out=bgr_ps[:], lhsT=ones[:], rhs=bias_rows[:, 1, :], start=True, stop=True)
+        brel = keep.tile([P, PACK], F32)
+        nc.vector.tensor_copy(out=brel[:], in_=brel_t[:])
         nc.vector.quantize_mx(
             out=x_codes[:].bitcast(FP8X4), scales=x_scales[:], in_=x_grouped[:].rearrange("p r t -> p (r t)")
         )
         x_mx = (x_codes[:], x_scales[:])
 
-        brel_t = setup_ps.tile([P, PACK], F32, tag="setup")
-        for t in range(PACK):
-            nc.tensor.matmul(
-                out=brel_t[:, t : t + 1], lhsT=bias_rows[:, 2, t:F:PACK], rhs=ones[:, 0:1], start=True, stop=True
-            )
-        bgr_ps = setup_ps.tile([P, F], F32, tag="setup")
-        nc.tensor.matmul(out=bgr_ps[:], lhsT=ones[:], rhs=bias_rows[:, 0, :], start=True, stop=True)
-        bgo_ps = setup_ps.tile([P, F], F32, tag="setup")
-        nc.tensor.matmul(out=bgo_ps[:], lhsT=ones[:], rhs=bias_rows[:, 1, :], start=True, stop=True)
+        def regroup_in_psum(raw, part, pool, tag):
+            bank = pool.tile([P, HALF, PACK], BF16, tag=tag)
+            for q in range(2):
+                first = part * HALF + q * P
+                nc.tensor.matmul(
+                    out=bank[:, q * P : (q + 1) * P, :],
+                    lhsT=ident_bf[:],
+                    rhs=raw[:, :, first : first + P].rearrange("p t n -> p n t"),
+                    start=True,
+                    stop=True,
+                )
+            return bank
 
-        rb_grouped = regroup_by_channel(keep, nc.scalar.copy, rb_raw, "rb_grouped")
+        def halves(grouped):
+            return grouped[:, 0:HALF, :], grouped[:, HALF:F, :]
 
-        xj_codes = keep.tile([P, TOKENS * I_PER_TILE], U32, align_bytes=64)
-        xj_scales = keep.tile([P, TOKENS * I_PER_TILE], U8, align_bytes=64)
-        nc.vector.tensor_copy(
-            out=xj_codes[:].bitcast(I32).rearrange("p (b c j) -> p b c j", b=BATCH, c=I_PER_TILE),
-            in_=x_codes[:]
-            .bitcast(I32)
-            .rearrange("p (b j) -> p b j", b=BATCH)
-            .unsqueeze(2)
-            .to_broadcast([P, BATCH, I_PER_TILE, NODES]),
-        )
-        nc.vector.tensor_copy(
-            out=xj_scales[:].bitcast(I32).rearrange("p (b c w) -> p b c w", b=BATCH, c=I_PER_TILE),
-            in_=x_scales[:]
-            .bitcast(I32)
-            .rearrange("p (b w) -> p b w", b=BATCH)
-            .unsqueeze(2)
-            .to_broadcast([P, BATCH, I_PER_TILE, NODES // BYTES_PER_WORD]),
-        )
-        xj = (xj_codes, xj_scales)
-        nc.vector.quantize_mx(
-            out=x4_codes[:].bitcast(FP8X4),
-            scales=x4_scales[:],
-            in_=x_fourfold[:].rearrange("p r c t -> p (r c t)"),
-        )
-        brel = keep.tile([P, PACK], F32)
-        nc.vector.tensor_copy(out=brel[:], in_=brel_t[:])
-
-        xi_codes = keep.tile([P, PAIRS], U32, align_bytes=64)
-        xi_scales = keep.tile([P, PAIRS], U8, align_bytes=64)
-        xi = (xi_codes, xi_scales)
-        repeats = NODES // BYTES_PER_WORD
-
-        def repeat_xi(b):
-            tokens = slice(b * NODES, (b + 1) * NODES)
-            nc.vector.tensor_copy(
-                out=xi_codes[:]
-                .bitcast(I32)
-                .rearrange("p (r e c) -> p r e c", e=repeats, c=BYTES_PER_WORD)[:, tokens, :, :],
-                in_=x4_codes[:]
-                .bitcast(I32)
-                .rearrange("p (r c) -> p r c", c=BYTES_PER_WORD)[:, tokens, :]
-                .unsqueeze(2)
-                .to_broadcast([P, NODES, repeats, BYTES_PER_WORD]),
-            )
-            nc.vector.tensor_copy(
-                out=xi_scales[:].bitcast(I32).rearrange("p (r e) -> p r e", e=repeats)[:, tokens, :],
-                in_=x4_scales[:].bitcast(I32)[:, tokens].unsqueeze(2).to_broadcast([P, NODES, repeats]),
-            )
-
-        ra_grouped = regroup_by_channel(keep, nc.vector.tensor_copy, ra_raw, "ra_grouped")
         rb = quantise_weight(nc, keep, rb_grouped, "rb")
         b_t = setup_ps.tile([P, PACK, TOKENS], F32, tag="setup")
         for t in range(PACK):
             mx_pass(nc, b_t[:, t, :], columns(rb, t * P, P), x_mx, start=True, stop=True)
+        regroup_by_channel(nc.vector.tensor_copy, ra_grouped, ra_raw, 0, 2)
+        regroup_by_channel(nc.scalar.copy, ra_grouped, ra_raw, 2, 4)
         ra = quantise_weight(nc, keep, ra_grouped, "ra")
-        a_t = keep_ps.tile([P, PACK, TOKENS], F32)
-        for t in range(PACK):
-            mx_pass(nc, a_t[:, t, :], columns(ra, t * P, P), x_mx, start=True, stop=True)
-        repeat_xi(0)
+        gc_grouped = new_grouped(keep, "gc_grouped")
+        gb_grouped = new_grouped(keep, "gb_grouped")
+        ga_grouped = new_grouped(keep, "ga_grouped")
+        go_grouped = new_grouped(keep, "go_grouped")
+        gc_banks = [regroup_in_psum(gc_raw, part, acc_ps, "acc") for part in range(2)]
         b_plus = keep.tile([P, TOKENS, PACK], F32)
         nc.vector.tensor_tensor(
             out=b_plus[:],
@@ -228,97 +186,141 @@ def tile_languagemsgencoder_pa_kernel(
             in1=brel[:].unsqueeze(1).to_broadcast([P, TOKENS, PACK]),
             op=ADD,
         )
+        a_t = keep_ps.tile([P, PACK, TOKENS], F32)
+        for t in range(PACK):
+            mx_pass(nc, a_t[:, t, :], columns(ra, t * P, P), x_mx, start=True, stop=True)
         a_sb = keep.tile([P, TOKENS, PACK], F32)
-        nc.vector.tensor_copy(out=a_sb[:], in_=a_t[:].rearrange("p t r -> p r t"))
-        ga_grouped = regroup_weight(keep, nc.scalar.copy, ga_raw, "ga_grouped")
-        gb_grouped = regroup_weight(keep, nc.scalar.copy, gb_raw, "gb_grouped")
-        gc_grouped = regroup_weight(keep, nc.scalar.copy, gc_raw, "gc_grouped")
-        bgr = keep.tile([P, F], F32)
-        nc.scalar.copy(out=bgr[:], in_=bgr_ps[:])
-        go_grouped = regroup_weight(keep, nc.scalar.copy, go_raw, "go_grouped")
-        bgo = keep.tile([P, F], F32)
-        nc.scalar.copy(out=bgo[:], in_=bgo_ps[:])
+        nc.scalar.copy(out=a_sb[:], in_=a_t[:].rearrange("p t r -> p r t"))
+        for part in range(2):
+            nc.scalar.copy(out=halves(gc_grouped)[part], in_=gc_banks[part][:])
 
         rel0_codes = keep.tile([P, PAIRS], U32, align_bytes=64)
         rel0_scales = keep.tile([P, PAIRS], U8, align_bytes=64)
         rel0_mx = (rel0_codes, rel0_scales)
+        xj_codes = keep.tile([P, PAIRS], U32, align_bytes=64)
+        xj_scales = keep.tile([P, PAIRS], U8, align_bytes=64)
+        xj = (xj_codes, xj_scales)
 
-        def form_rel0(chunk, gpsimd_i):
-            first_token = chunk * I_PER_CHUNK
-            b = first_token // NODES
-            rel0 = stream.tile([P, I_PER_CHUNK, NODES, PACK], BF16, align_bytes=64)
-            b_part = b_plus[:, b * NODES : (b + 1) * NODES, :].unsqueeze(1)
-            nc.gpsimd.tensor_tensor(
-                out=rel0[:, 0:gpsimd_i, :, :],
-                in0=a_sb[:, first_token : first_token + gpsimd_i, :]
+        def repeat_xj(first_j, last_j):
+            count = last_j - first_j
+            nc.vector.tensor_copy(
+                out=xj_codes[:].bitcast(I32).rearrange("p (j i b) -> p j i b", i=NODES, b=BATCH)[:, first_j:last_j, :, :],
+                in_=x_codes[:]
+                .bitcast(I32)
+                .rearrange("p (j b) -> p j b", b=BATCH)[:, first_j:last_j, :]
                 .unsqueeze(2)
-                .to_broadcast([P, gpsimd_i, NODES, PACK]),
-                in1=b_part.to_broadcast([P, gpsimd_i, NODES, PACK]),
+                .to_broadcast([P, count, NODES, BATCH]),
+            )
+            nc.vector.tensor_copy(
+                out=xj_scales[:].bitcast(I32).rearrange("p (j i) -> p j i", i=NODES)[:, first_j:last_j, :],
+                in_=x_scales[:].bitcast(I32)[:, first_j:last_j].unsqueeze(2).to_broadcast([P, count, NODES]),
+            )
+
+        a_view = a_t[:].rearrange("p t r -> p r t")
+
+        def add_pairs(engine, rel0, a_part, first_j, size, first_i, last_i):
+            shape = [P, size, last_i - first_i, BATCH, PACK]
+            tokens = slice(first_i * BATCH, last_i * BATCH)
+            engine.tensor_tensor(
+                out=rel0[:, 0:size, tokens, :].rearrange("p j (i b) t -> p j i b t", b=BATCH),
+                in0=a_part[:, tokens, :].rearrange("p (i b) t -> p i b t", b=BATCH).unsqueeze(1).to_broadcast(shape),
+                in1=b_plus[:]
+                .rearrange("p (j b) t -> p j b t", b=BATCH)[:, first_j : first_j + size, :, :]
+                .unsqueeze(2)
+                .to_broadcast(shape),
                 op=ADD,
             )
-            vector_i = I_PER_CHUNK - gpsimd_i
-            nc.vector.tensor_tensor(
-                out=rel0[:, gpsimd_i:I_PER_CHUNK, :, :],
-                in0=a_t[:, :, first_token + gpsimd_i : first_token + I_PER_CHUNK]
-                .rearrange("p t i -> p i t")
-                .unsqueeze(2)
-                .to_broadcast([P, vector_i, NODES, PACK]),
-                in1=b_part.to_broadcast([P, vector_i, NODES, PACK]),
-                op=ADD,
-            )
+
+        def form_rel0(first_j, size):
+            rel0 = stream.tile([P, MAX_CHUNK, TOKENS, PACK], BF16, align_bytes=64)
+            add_pairs(nc.gpsimd, rel0, a_sb, first_j, size, 0, GPSIMD_I)
+            add_pairs(nc.vector, rel0, a_view, first_j, size, GPSIMD_I, NODES)
             return rel0
 
-        def quantise_rel0(chunk, rel0):
-            chunk_codes, chunk_scales = columns(rel0_mx, chunk * COLS_PER_CHUNK, COLS_PER_CHUNK)
+        def quantise_rel0(rel0, first_j, size):
+            codes, scales = columns(rel0_mx, first_j * TOKENS, size * TOKENS)
             nc.vector.quantize_mx(
-                out=chunk_codes.bitcast(FP8X4), scales=chunk_scales, in_=rel0[:].rearrange("p i j t -> p (i j t)")
+                out=codes.bitcast(FP8X4),
+                scales=scales,
+                in_=rel0[:, 0:size, :, :].rearrange("p s r t -> p (s r t)"),
             )
 
-        def open_tile(first_row):
-            b = first_row // (NODES * NODES)
-            acc = acc_ps.tile([P, F], F32)
-            mx_pass(nc, acc[:], columns(xi, first_row, P), columns(ga, 0, F), start=True, stop=False)
-            mx_pass(nc, acc[:], columns(xj, b * P, P), columns(gb, 0, F), start=False, stop=False)
+        def open_tile(j):
+            acc = acc_ps.tile([P, F], F32, tag="acc")
+            mx_pass(nc, acc[:], columns(xj, j * TOKENS, TOKENS), columns(gb, 0, F), start=True, stop=False)
             return acc
 
-        def close_tile(acc, first_row):
-            mx_pass(nc, acc[:], columns(rel0_mx, first_row, P), columns(gc, 0, F), start=False, stop=True)
+        def close_tile(acc, j):
+            mx_pass(nc, acc[:], columns(rel0_mx, j * TOKENS, TOKENS), columns(gc, 0, F), start=False, stop=True)
 
-        def finish(acc, bias, rows):
-            result = results.tile([P, F], F32)
-            nc.vector.tensor_tensor(out=result[:], in0=acc[:], in1=bias[:], op=ADD)
-            nc.scalar.activation(out=result[:], in_=result[:], func=TANH)
-            nc.sync.dma_start(out=rows, in_=result[:])
+        def finish(acc, addend, result):
+            nc.vector.tensor_tensor(out=result, in0=acc[:], in1=addend[:], op=ADD)
+            nc.scalar.activation(out=result, in_=result, func=TANH)
 
-        def first_row_of(chunk, n):
-            return chunk * COLS_PER_CHUNK + n * P
-
-        def finish_rel(chunk, n, acc):
-            finish(acc, bgr, rel_rows[first_row_of(chunk, n) : first_row_of(chunk, n) + P, :])
-
-        rel0 = form_rel0(0, I_PER_CHUNK - GPSIMD_I)
-        ga = quantise_weight(nc, keep, ga_grouped, "ga")
-        gb = quantise_weight(nc, keep, gb_grouped, "gb")
-        accs = [open_tile(first_row_of(0, n)) for n in range(TILES_PER_CHUNK)]
+        starts = [sum(CHUNKS[:c]) for c in range(len(CHUNKS))]
+        rel0 = form_rel0(0, CHUNKS[0])
+        repeat_xj(0, starts[2])
+        gb_banks = [regroup_in_psum(gb_raw, part, acc_ps, "acc") for part in range(2)]
+        for part in range(2):
+            nc.vector.tensor_copy(out=halves(gb_grouped)[part], in_=gb_banks[part][:])
+        quantise_rel0(rel0, 0, CHUNKS[0])
         gc = quantise_weight(nc, keep, gc_grouped, "gc")
-        quantise_rel0(0, rel0)
-        for n in range(TILES_PER_CHUNK):
-            close_tile(accs[n], first_row_of(0, n))
+        gb = quantise_weight(nc, keep, gb_grouped, "gb")
+        ga_banks = [regroup_in_psum(ga_raw, part, setup_ps, "setup") for part in range(2)]
+        for part in range(2):
+            nc.scalar.copy(out=halves(ga_grouped)[part], in_=ga_banks[part][:])
+        bgr = keep.tile([P, F], F32)
+        nc.scalar.copy(out=bgr[:], in_=bgr_ps[:])
+        accs = {j: open_tile(j) for j in range(CHUNKS[0])}
+        for j in range(CHUNKS[0]):
+            close_tile(accs[j], j)
+        rel0 = form_rel0(starts[1], CHUNKS[1])
+        for j in range(starts[1], starts[1] + 2):
+            accs[j] = open_tile(j)
+        ga = quantise_weight(nc, keep, ga_grouped, "ga")
+        c_ps = setup_ps.tile([P, F], F32, tag="setup")
+        mx_pass(nc, c_ps[:], x_mx, columns(ga, 0, F), start=True, stop=True)
+        quantise_rel0(rel0, starts[1], CHUNKS[1])
+        for j in range(starts[1], starts[1] + 2):
+            close_tile(accs[j], j)
+        c_gr = keep.tile([P, F], F32)
+        nc.vector.tensor_tensor(out=c_gr[:], in0=c_ps[:], in1=bgr[:], op=ADD)
 
-        for chunk in range(1, CHUNKS):
-            rel0 = form_rel0(chunk, GPSIMD_I)
-            for n in range(TILES_PER_CHUNK):
-                finish_rel(chunk - 1, n, accs[n])
-                accs[n] = open_tile(first_row_of(chunk, n))
-            if (chunk + 1) % CHUNKS_PER_BATCH == 0 and chunk + 1 < CHUNKS:
-                repeat_xi((chunk + 1) // CHUNKS_PER_BATCH)
-            quantise_rel0(chunk, rel0)
-            for n in range(TILES_PER_CHUNK):
-                close_tile(accs[n], first_row_of(chunk, n))
-
-        go = quantise_weight(nc, keep, go_grouped, "go")
-        new_x_acc = setup_ps.tile([P, F], F32, tag="setup")
-        mx_pass(nc, new_x_acc[:], x_mx, columns(go, 0, F), start=True, stop=True)
-        for n in range(TILES_PER_CHUNK):
-            finish_rel(CHUNKS - 1, n, accs[n])
-        finish(new_x_acc, bgo, new_x_rows)
+        opened, closed = starts[1] + 2, starts[1] + 2
+        for chunk in range(1, len(CHUNKS) + 1):
+            first, size = (starts[chunk], CHUNKS[chunk]) if chunk < len(CHUNKS) else (NODES, 0)
+            if 1 < chunk < len(CHUNKS):
+                rel0 = form_rel0(first, size)
+            previous = CHUNKS[chunk - 1]
+            result = results.tile([P, MAX_CHUNK, F], F32)
+            for j in range(first - previous, first):
+                finish(accs[j], c_gr, result[:, j - first + previous, :])
+                if opened < first + size:
+                    accs[opened] = open_tile(opened)
+                    opened += 1
+            for b in range(BATCH):
+                nc.sync.dma_start(
+                    out=out_1[b, :, first - previous : first, :], in_=result[b:P:BATCH, 0:previous, :]
+                )
+            if chunk + 1 < len(CHUNKS):
+                repeat_xj(first + size, first + size + CHUNKS[chunk + 1])
+            if 1 < chunk < len(CHUNKS):
+                quantise_rel0(rel0, first, size)
+            while closed < first + size:
+                close_tile(accs[closed], closed)
+                closed += 1
+            if chunk == 1:
+                regroup(nc.scalar.copy, go_grouped, go_raw)
+            if chunk == 4:
+                go = quantise_weight(nc, keep, go_grouped, "go")
+                bgo_ps = setup_ps.tile([P, F], F32, tag="setup")
+                nc.tensor.matmul(out=bgo_ps[:], lhsT=ones[:], rhs=bias_rows[:, 2, :], start=True, stop=True)
+                bgo = keep.tile([P, F], F32)
+                nc.scalar.copy(out=bgo[:], in_=bgo_ps[:])
+                new_x_acc = setup_ps.tile([P, F], F32, tag="setup")
+                mx_pass(nc, new_x_acc[:], x_mx, columns(go, 0, F), start=True, stop=True)
+            if chunk == 5:
+                new_x = keep.tile([P, F], F32)
+                finish(new_x_acc, bgo, new_x[:])
+                for b in range(BATCH):
+                    nc.sync.dma_start(out=out_0[b], in_=new_x[b:P:BATCH, :])

@@ -20,7 +20,6 @@ TOKENS = BATCH * NODES
 D = P * PACK
 F = 512
 PAIRS = BATCH * NODES * NODES
-HALF = F // 2
 
 CHUNKS = [2, 4, 4, 4, 4, 4, 4, 4, 2]
 MAX_CHUNK = max(CHUNKS)
@@ -105,8 +104,6 @@ def tile_languagemsgencoder_pa_kernel(
         nc.vector.memset(bias_rows[:].rearrange("p a f -> p (a f)").bitcast(I32), 0)
         ones = keep.tile([P, P], BF16)
         nc.vector.memset(ones[:], 1.0)
-        ident_bf = keep.tile([P, P], BF16)
-        nc.vector.tensor_copy(out=ident_bf[:], in_=ident[:])
 
         x_sb = keep.tile([P, D], BF16)
         for b in range(BATCH):
@@ -151,22 +148,6 @@ def tile_languagemsgencoder_pa_kernel(
         )
         x_mx = (x_codes[:], x_scales[:])
 
-        def regroup_in_psum(raw, part, pool, tag):
-            bank = pool.tile([P, HALF, PACK], BF16, tag=tag)
-            for q in range(2):
-                first = part * HALF + q * P
-                nc.tensor.matmul(
-                    out=bank[:, q * P : (q + 1) * P, :],
-                    lhsT=ident_bf[:],
-                    rhs=raw[:, :, first : first + P].rearrange("p t n -> p n t"),
-                    start=True,
-                    stop=True,
-                )
-            return bank
-
-        def halves(grouped):
-            return grouped[:, 0:HALF, :], grouped[:, HALF:F, :]
-
         rb = quantise_weight(nc, keep, rb_grouped, "rb")
         b_t = setup_ps.tile([P, PACK, TOKENS], F32, tag="setup")
         for t in range(PACK):
@@ -178,7 +159,6 @@ def tile_languagemsgencoder_pa_kernel(
         gb_grouped = new_grouped(keep, "gb_grouped")
         ga_grouped = new_grouped(keep, "ga_grouped")
         go_grouped = new_grouped(keep, "go_grouped")
-        gc_banks = [regroup_in_psum(gc_raw, part, acc_ps, "acc") for part in range(2)]
         b_plus = keep.tile([P, TOKENS, PACK], F32)
         nc.vector.tensor_tensor(
             out=b_plus[:],
@@ -191,8 +171,7 @@ def tile_languagemsgencoder_pa_kernel(
             mx_pass(nc, a_t[:, t, :], columns(ra, t * P, P), x_mx, start=True, stop=True)
         a_sb = keep.tile([P, TOKENS, PACK], F32)
         nc.scalar.copy(out=a_sb[:], in_=a_t[:].rearrange("p t r -> p r t"))
-        for part in range(2):
-            nc.scalar.copy(out=halves(gc_grouped)[part], in_=gc_banks[part][:])
+        regroup(nc.scalar.copy, gc_grouped, gc_raw)
 
         rel0_codes = keep.tile([P, PAIRS], U32, align_bytes=64)
         rel0_scales = keep.tile([P, PAIRS], U8, align_bytes=64)
@@ -260,15 +239,11 @@ def tile_languagemsgencoder_pa_kernel(
         starts = [sum(CHUNKS[:c]) for c in range(len(CHUNKS))]
         rel0 = form_rel0(0, CHUNKS[0])
         repeat_xj(0, starts[2])
-        gb_banks = [regroup_in_psum(gb_raw, part, acc_ps, "acc") for part in range(2)]
-        for part in range(2):
-            nc.vector.tensor_copy(out=halves(gb_grouped)[part], in_=gb_banks[part][:])
+        regroup(nc.vector.tensor_copy, gb_grouped, gb_raw)
         quantise_rel0(rel0, 0, CHUNKS[0])
         gc = quantise_weight(nc, keep, gc_grouped, "gc")
         gb = quantise_weight(nc, keep, gb_grouped, "gb")
-        ga_banks = [regroup_in_psum(ga_raw, part, setup_ps, "setup") for part in range(2)]
-        for part in range(2):
-            nc.scalar.copy(out=halves(ga_grouped)[part], in_=ga_banks[part][:])
+        regroup(nc.scalar.copy, ga_grouped, ga_raw)
         bgr = keep.tile([P, F], F32)
         nc.scalar.copy(out=bgr[:], in_=bgr_ps[:])
         accs = {j: open_tile(j) for j in range(CHUNKS[0])}

@@ -21,6 +21,8 @@ D = P * PACK
 F = 512
 PAIRS = BATCH * NODES * NODES
 
+HALF = F // 2
+
 CHUNKS = [2, 4, 4, 4, 4, 4, 4, 4, 2]
 MAX_CHUNK = max(CHUNKS)
 GPSIMD_I = 20
@@ -148,31 +150,6 @@ def tile_languagemsgencoder_pa_kernel(
         )
         x_mx = (x_codes[:], x_scales[:])
 
-        rb = quantise_weight(nc, keep, rb_grouped, "rb")
-        b_t = setup_ps.tile([P, PACK, TOKENS], F32, tag="setup")
-        for t in range(PACK):
-            mx_pass(nc, b_t[:, t, :], columns(rb, t * P, P), x_mx, start=True, stop=True)
-        regroup_by_channel(nc.vector.tensor_copy, ra_grouped, ra_raw, 0, 2)
-        regroup_by_channel(nc.scalar.copy, ra_grouped, ra_raw, 2, 4)
-        ra = quantise_weight(nc, keep, ra_grouped, "ra")
-        gc_grouped = new_grouped(keep, "gc_grouped")
-        gb_grouped = new_grouped(keep, "gb_grouped")
-        ga_grouped = new_grouped(keep, "ga_grouped")
-        go_grouped = new_grouped(keep, "go_grouped")
-        b_plus = keep.tile([P, TOKENS, PACK], F32)
-        nc.vector.tensor_tensor(
-            out=b_plus[:],
-            in0=b_t[:].rearrange("p t r -> p r t"),
-            in1=brel[:].unsqueeze(1).to_broadcast([P, TOKENS, PACK]),
-            op=ADD,
-        )
-        a_t = keep_ps.tile([P, PACK, TOKENS], F32)
-        for t in range(PACK):
-            mx_pass(nc, a_t[:, t, :], columns(ra, t * P, P), x_mx, start=True, stop=True)
-        a_sb = keep.tile([P, TOKENS, PACK], F32)
-        nc.scalar.copy(out=a_sb[:], in_=a_t[:].rearrange("p t r -> p r t"))
-        regroup(nc.scalar.copy, gc_grouped, gc_raw)
-
         rel0_codes = keep.tile([P, PAIRS], U32, align_bytes=64)
         rel0_scales = keep.tile([P, PAIRS], U8, align_bytes=64)
         rel0_mx = (rel0_codes, rel0_scales)
@@ -194,6 +171,38 @@ def tile_languagemsgencoder_pa_kernel(
                 out=xj_scales[:].bitcast(I32).rearrange("p (j i) -> p j i", i=NODES)[:, first_j:last_j, :],
                 in_=x_scales[:].bitcast(I32)[:, first_j:last_j].unsqueeze(2).to_broadcast([P, count, NODES]),
             )
+
+        rb = quantise_weight(nc, keep, rb_grouped, "rb")
+        b_t = setup_ps.tile([P, PACK, TOKENS], F32, tag="setup")
+        for t in range(PACK):
+            mx_pass(nc, b_t[:, t, :], columns(rb, t * P, P), x_mx, start=True, stop=True)
+        regroup_by_channel(nc.vector.tensor_copy, ra_grouped, ra_raw, 0, 2)
+        regroup_by_channel(nc.scalar.copy, ra_grouped, ra_raw, 2, 4)
+        ra = quantise_weight(nc, keep, ra_grouped, "ra")
+        gc_grouped = new_grouped(keep, "gc_grouped")
+        gb_grouped = new_grouped(keep, "gb_grouped")
+        ga_grouped = new_grouped(keep, "ga_grouped")
+        go_grouped = new_grouped(keep, "go_grouped")
+        b_plus = keep.tile([P, TOKENS, PACK], F32)
+        nc.vector.tensor_tensor(
+            out=b_plus[:],
+            in0=b_t[:].rearrange("p t r -> p r t"),
+            in1=brel[:].unsqueeze(1).to_broadcast([P, TOKENS, PACK]),
+            op=ADD,
+        )
+        regroup(nc.scalar.copy, gc_grouped, gc_raw, 0, HALF)
+        starts = [sum(CHUNKS[:c]) for c in range(len(CHUNKS))]
+        repeat_xj(0, starts[2])
+        regroup(nc.vector.tensor_copy, gb_grouped, gb_raw)
+        a_t = keep_ps.tile([P, PACK, TOKENS], F32)
+        for t in range(PACK):
+            mx_pass(nc, a_t[:, t, :], columns(ra, t * P, P), x_mx, start=True, stop=True)
+        a_sb = keep.tile([P, TOKENS, PACK], F32)
+        nc.scalar.copy(out=a_sb[:], in_=a_t[:].rearrange("p t r -> p r t"))
+        regroup(nc.scalar.copy, gc_grouped, gc_raw, HALF, F)
+        regroup(nc.scalar.copy, ga_grouped, ga_raw, 0, HALF)
+        bgr = keep.tile([P, F], F32)
+        nc.scalar.copy(out=bgr[:], in_=bgr_ps[:])
 
         a_view = a_t[:].rearrange("p t r -> p r t")
 
@@ -236,35 +245,24 @@ def tile_languagemsgencoder_pa_kernel(
             nc.vector.tensor_tensor(out=result, in0=acc[:], in1=addend[:], op=ADD)
             nc.scalar.activation(out=result, in_=result, func=TANH)
 
-        starts = [sum(CHUNKS[:c]) for c in range(len(CHUNKS))]
         rel0 = form_rel0(0, CHUNKS[0])
-        repeat_xj(0, starts[2])
-        regroup(nc.vector.tensor_copy, gb_grouped, gb_raw)
-        quantise_rel0(rel0, 0, CHUNKS[0])
-        gc = quantise_weight(nc, keep, gc_grouped, "gc")
         gb = quantise_weight(nc, keep, gb_grouped, "gb")
-        regroup(nc.scalar.copy, ga_grouped, ga_raw)
-        bgr = keep.tile([P, F], F32)
-        nc.scalar.copy(out=bgr[:], in_=bgr_ps[:])
-        accs = {j: open_tile(j) for j in range(CHUNKS[0])}
-        for j in range(CHUNKS[0]):
-            close_tile(accs[j], j)
-        rel0 = form_rel0(starts[1], CHUNKS[1])
-        for j in range(starts[1], starts[1] + 2):
-            accs[j] = open_tile(j)
+        accs = {j: open_tile(j) for j in range(CHUNKS[0] + 2)}
+        gc = quantise_weight(nc, keep, gc_grouped, "gc")
+        regroup(nc.vector.tensor_copy, ga_grouped, ga_raw, HALF, F)
         ga = quantise_weight(nc, keep, ga_grouped, "ga")
         c_ps = setup_ps.tile([P, F], F32, tag="setup")
         mx_pass(nc, c_ps[:], x_mx, columns(ga, 0, F), start=True, stop=True)
-        quantise_rel0(rel0, starts[1], CHUNKS[1])
-        for j in range(starts[1], starts[1] + 2):
+        quantise_rel0(rel0, 0, CHUNKS[0])
+        for j in range(CHUNKS[0]):
             close_tile(accs[j], j)
         c_gr = keep.tile([P, F], F32)
         nc.vector.tensor_tensor(out=c_gr[:], in0=c_ps[:], in1=bgr[:], op=ADD)
 
-        opened, closed = starts[1] + 2, starts[1] + 2
+        opened, closed = CHUNKS[0] + 2, CHUNKS[0]
         for chunk in range(1, len(CHUNKS) + 1):
             first, size = (starts[chunk], CHUNKS[chunk]) if chunk < len(CHUNKS) else (NODES, 0)
-            if 1 < chunk < len(CHUNKS):
+            if chunk < len(CHUNKS):
                 rel0 = form_rel0(first, size)
             previous = CHUNKS[chunk - 1]
             result = results.tile([P, MAX_CHUNK, F], F32)
@@ -279,7 +277,7 @@ def tile_languagemsgencoder_pa_kernel(
                 )
             if chunk + 1 < len(CHUNKS):
                 repeat_xj(first + size, first + size + CHUNKS[chunk + 1])
-            if 1 < chunk < len(CHUNKS):
+            if chunk < len(CHUNKS):
                 quantise_rel0(rel0, first, size)
             while closed < first + size:
                 close_tile(accs[closed], closed)

@@ -23,9 +23,11 @@ PAIRS = BATCH * NODES * NODES
 
 HALF = F // 2
 
+BYTES_PER_WORD = 4
+WORDS = NODES // BYTES_PER_WORD
 CHUNKS = [2, 4, 4, 4, 4, 4, 4, 4, 2]
 MAX_CHUNK = max(CHUNKS)
-GPSIMD_I = 20
+GPSIMD_B = 3
 
 
 FLOPS = 2 * (5 * TOKENS * D * F + PAIRS * D * F)
@@ -85,6 +87,7 @@ def tile_languagemsgencoder_pa_kernel(
     tc, text_embedding, W_rel, b_rel, W_go, b_go, W_gr, b_gr, out_0, out_1
 ):
     nc = tc.nc
+    rel_rows = out_1.rearrange("b i j f -> (b i) j f")
 
     with ExitStack() as ctx:
         keep = ctx.enter_context(tc.tile_pool(name="keep", bufs=1))
@@ -108,8 +111,7 @@ def tile_languagemsgencoder_pa_kernel(
         nc.vector.memset(ones[:], 1.0)
 
         x_sb = keep.tile([P, D], BF16)
-        for b in range(BATCH):
-            nc.sync.dma_start(out=x_sb[b:P:BATCH, :], in_=text_embedding[b])
+        nc.sync.dma_start(out=x_sb[:], in_=text_embedding.rearrange("b n d -> (b n) d"))
         rb_raw = load_weight(nc, keep, W_rel[D : 2 * D, :], "rb_raw")
         for row, bias in enumerate((b_rel, b_gr, b_go)):
             nc.sync.dma_start(out=bias_rows[0:1, row, :], in_=bias.rearrange("(o f) -> o f", o=1))
@@ -157,19 +159,26 @@ def tile_languagemsgencoder_pa_kernel(
         xj_scales = keep.tile([P, PAIRS], U8, align_bytes=64)
         xj = (xj_codes, xj_scales)
 
+        x4_scales = keep.tile([P, TOKENS, BYTES_PER_WORD], U8, align_bytes=64)
+        for c in range(BYTES_PER_WORD):
+            nc.gpsimd.tensor_copy(out=x4_scales[:, :, c], in_=x_scales[:])
+        x4_words = x4_scales[:].rearrange("p r c -> p (r c)").bitcast(I32)
+
         def repeat_xj(first_j, last_j):
             count = last_j - first_j
             nc.vector.tensor_copy(
-                out=xj_codes[:].bitcast(I32).rearrange("p (j i b) -> p j i b", i=NODES, b=BATCH)[:, first_j:last_j, :, :],
+                out=xj_codes[:].bitcast(I32).rearrange("p (j b i) -> p j b i", b=BATCH, i=NODES)[:, first_j:last_j, :, :],
                 in_=x_codes[:]
                 .bitcast(I32)
-                .rearrange("p (j b) -> p j b", b=BATCH)[:, first_j:last_j, :]
-                .unsqueeze(2)
-                .to_broadcast([P, count, NODES, BATCH]),
+                .rearrange("p (b j) -> p j b", b=BATCH)[:, first_j:last_j, :]
+                .unsqueeze(3)
+                .to_broadcast([P, count, BATCH, NODES]),
             )
             nc.vector.tensor_copy(
-                out=xj_scales[:].bitcast(I32).rearrange("p (j i) -> p j i", i=NODES)[:, first_j:last_j, :],
-                in_=x_scales[:].bitcast(I32)[:, first_j:last_j].unsqueeze(2).to_broadcast([P, count, NODES]),
+                out=xj_scales[:].bitcast(I32).rearrange("p (j b w) -> p j b w", b=BATCH, w=WORDS)[:, first_j:last_j, :, :],
+                in_=x4_words.rearrange("p (b j) -> p j b", b=BATCH)[:, first_j:last_j, :]
+                .unsqueeze(3)
+                .to_broadcast([P, count, BATCH, WORDS]),
             )
 
         rb = quantise_weight(nc, keep, rb_grouped, "rb")
@@ -206,23 +215,23 @@ def tile_languagemsgencoder_pa_kernel(
 
         a_view = a_t[:].rearrange("p t r -> p r t")
 
-        def add_pairs(engine, rel0, a_part, first_j, size, first_i, last_i):
-            shape = [P, size, last_i - first_i, BATCH, PACK]
-            tokens = slice(first_i * BATCH, last_i * BATCH)
+        def add_pairs(engine, rel0, a_part, first_j, size, b):
+            shape = [P, size, NODES, PACK]
+            tokens = slice(b * NODES, (b + 1) * NODES)
             engine.tensor_tensor(
-                out=rel0[:, 0:size, tokens, :].rearrange("p j (i b) t -> p j i b t", b=BATCH),
-                in0=a_part[:, tokens, :].rearrange("p (i b) t -> p i b t", b=BATCH).unsqueeze(1).to_broadcast(shape),
-                in1=b_plus[:]
-                .rearrange("p (j b) t -> p j b t", b=BATCH)[:, first_j : first_j + size, :, :]
-                .unsqueeze(2)
-                .to_broadcast(shape),
+                out=rel0[:, 0:size, tokens, :],
+                in0=a_part[:, tokens, :].unsqueeze(1).to_broadcast(shape),
+                in1=b_plus[:, b * NODES + first_j : b * NODES + first_j + size, :].unsqueeze(2).to_broadcast(shape),
                 op=ADD,
             )
 
         def form_rel0(first_j, size):
             rel0 = stream.tile([P, MAX_CHUNK, TOKENS, PACK], BF16, align_bytes=64)
-            add_pairs(nc.gpsimd, rel0, a_sb, first_j, size, 0, GPSIMD_I)
-            add_pairs(nc.vector, rel0, a_view, first_j, size, GPSIMD_I, NODES)
+            for b in range(BATCH):
+                if b < GPSIMD_B:
+                    add_pairs(nc.gpsimd, rel0, a_sb, first_j, size, b)
+                else:
+                    add_pairs(nc.vector, rel0, a_view, first_j, size, b)
             return rel0
 
         def quantise_rel0(rel0, first_j, size):
@@ -271,10 +280,7 @@ def tile_languagemsgencoder_pa_kernel(
                 if opened < first + size:
                     accs[opened] = open_tile(opened)
                     opened += 1
-            for b in range(BATCH):
-                nc.sync.dma_start(
-                    out=out_1[b, :, first - previous : first, :], in_=result[b:P:BATCH, 0:previous, :]
-                )
+            nc.sync.dma_start(out=rel_rows[:, first - previous : first, :], in_=result[:, 0:previous, :])
             if chunk + 1 < len(CHUNKS):
                 repeat_xj(first + size, first + size + CHUNKS[chunk + 1])
             if chunk < len(CHUNKS):
@@ -295,5 +301,4 @@ def tile_languagemsgencoder_pa_kernel(
             if chunk == 5:
                 new_x = keep.tile([P, F], F32)
                 finish(new_x_acc, bgo, new_x[:])
-                for b in range(BATCH):
-                    nc.sync.dma_start(out=out_0[b], in_=new_x[b:P:BATCH, :])
+                nc.sync.dma_start(out=out_0.rearrange("b n f -> (b n) f"), in_=new_x[:])

@@ -27,7 +27,10 @@ BYTES_PER_WORD = 4
 WORDS = NODES // BYTES_PER_WORD
 CHUNKS = [2, 4, 4, 4, 4, 4, 4, 4, 2]
 MAX_CHUNK = max(CHUNKS)
-GPSIMD_B = 3
+NEW_X_CHUNK = 5
+FLIPPED = (1, 2, 3, 4, 5, 6)
+ACC_BANKS = 3
+GPSIMD_TILES = {8: 4, 4: 2, 2: 1}
 
 
 FLOPS = 2 * (5 * TOKENS * D * F + PAIRS * D * F)
@@ -92,10 +95,11 @@ def tile_languagemsgencoder_pa_kernel(
     with ExitStack() as ctx:
         keep = ctx.enter_context(tc.tile_pool(name="keep", bufs=1))
         stream = ctx.enter_context(tc.tile_pool(name="stream", bufs=1))
-        results = ctx.enter_context(tc.tile_pool(name="results", bufs=3))
+        results = ctx.enter_context(tc.tile_pool(name="results", bufs=6))
+        flips = ctx.enter_context(tc.tile_pool(name="flips", bufs=2))
         keep_ps = ctx.enter_context(tc.psum_pool(name="keep_ps", bufs=1))
-        setup_ps = ctx.enter_context(tc.psum_pool(name="setup_ps", bufs=3))
-        acc_ps = ctx.enter_context(tc.psum_pool(name="acc_ps", bufs=4))
+        setup_ps = ctx.enter_context(tc.psum_pool(name="setup_ps", bufs=4))
+        acc_ps = ctx.enter_context(tc.psum_pool(name="acc_ps", bufs=ACC_BANKS))
         ctx.enter_context(tc.manual_schedule())
 
         warm = keep.tile([P, 1], F32)
@@ -138,19 +142,24 @@ def tile_languagemsgencoder_pa_kernel(
             out=x_grouped[:].rearrange("p r t -> p (r t)").bitcast(F32).rearrange("p (r u) -> p r u", u=2),
             in_=x_t[:].rearrange("p u r -> p r u"),
         )
-        brel_t = setup_ps.tile([P, PACK], F32, tag="setup")
+        bias_t = setup_ps.tile([P, 2 * PACK], F32, tag="setup")
         for t in range(PACK):
-            nc.tensor.matmul(
-                out=brel_t[:, t : t + 1], lhsT=bias_rows[:, 0, t:F:PACK], rhs=ones[:, 0:1], start=True, stop=True
-            )
+            for column, row in ((t, bias_rows[:, 0, t:F:PACK]), (PACK + t, bias_rows[:, 1, t * P : (t + 1) * P])):
+                nc.tensor.matmul(
+                    out=bias_t[:, column : column + 1], lhsT=row, rhs=ones[:, 0:1], start=True, stop=True
+                )
         bgr_ps = setup_ps.tile([P, F], F32, tag="setup")
         nc.tensor.matmul(out=bgr_ps[:], lhsT=ones[:], rhs=bias_rows[:, 1, :], start=True, stop=True)
-        brel = keep.tile([P, PACK], F32)
-        nc.vector.tensor_copy(out=brel[:], in_=brel_t[:])
+        bias_cols = keep.tile([P, 2 * PACK], F32)
+        nc.vector.tensor_copy(out=bias_cols[:], in_=bias_t[:])
+        brel = bias_cols[:, 0:PACK]
+        bgr_cols = bias_cols[:, PACK : 2 * PACK]
         nc.vector.quantize_mx(
             out=x_codes[:].bitcast(FP8X4), scales=x_scales[:], in_=x_grouped[:].rearrange("p r t -> p (r t)")
         )
         x_mx = (x_codes[:], x_scales[:])
+        x2_codes = keep.tile([P, 2 * TOKENS], U32, align_bytes=64)
+        x2_scales = keep.tile([P, 2 * TOKENS], U8, align_bytes=64)
 
         rel0_codes = keep.tile([P, PAIRS], U32, align_bytes=64)
         rel0_scales = keep.tile([P, PAIRS], U8, align_bytes=64)
@@ -161,7 +170,7 @@ def tile_languagemsgencoder_pa_kernel(
 
         x4_scales = keep.tile([P, TOKENS, BYTES_PER_WORD], U8, align_bytes=64)
         for c in range(BYTES_PER_WORD):
-            nc.gpsimd.tensor_copy(out=x4_scales[:, :, c], in_=x_scales[:])
+            nc.vector.tensor_copy(out=x4_scales[:, :, c], in_=x_scales[:])
         x4_words = x4_scales[:].rearrange("p r c -> p (r c)").bitcast(I32)
 
         def repeat_xj(first_j, last_j):
@@ -192,17 +201,25 @@ def tile_languagemsgencoder_pa_kernel(
         gb_grouped = new_grouped(keep, "gb_grouped")
         ga_grouped = new_grouped(keep, "ga_grouped")
         go_grouped = new_grouped(keep, "go_grouped")
-        b_plus = keep.tile([P, TOKENS, PACK], F32)
+        b_plus = keep.tile([P, NODES, BATCH, PACK], F32)
         nc.vector.tensor_tensor(
-            out=b_plus[:],
-            in0=b_t[:].rearrange("p t r -> p r t"),
-            in1=brel[:].unsqueeze(1).to_broadcast([P, TOKENS, PACK]),
+            out=b_plus[:].rearrange("p j b t -> p b j t"),
+            in0=b_t[:].rearrange("p t (b j) -> p b j t", b=BATCH),
+            in1=brel.unsqueeze(1).unsqueeze(1).to_broadcast([P, BATCH, NODES, PACK]),
             op=ADD,
         )
         regroup(nc.scalar.copy, gc_grouped, gc_raw, 0, HALF)
         starts = [sum(CHUNKS[:c]) for c in range(len(CHUNKS))]
         repeat_xj(0, starts[2])
         regroup(nc.vector.tensor_copy, gb_grouped, gb_raw)
+        nc.vector.tensor_copy(
+            out=x2_codes[:].bitcast(I32).rearrange("p (e r) -> p e r", e=2),
+            in_=x_codes[:].bitcast(I32).unsqueeze(1).to_broadcast([P, 2, TOKENS]),
+        )
+        nc.vector.tensor_copy(
+            out=x2_scales[:].bitcast(I32).rearrange("p (e r) -> p e r", e=2),
+            in_=x_scales[:].bitcast(I32).unsqueeze(1).to_broadcast([P, 2, TOKENS // BYTES_PER_WORD]),
+        )
         a_t = keep_ps.tile([P, PACK, TOKENS], F32)
         for t in range(PACK):
             mx_pass(nc, a_t[:, t, :], columns(ra, t * P, P), x_mx, start=True, stop=True)
@@ -212,26 +229,30 @@ def tile_languagemsgencoder_pa_kernel(
         regroup(nc.scalar.copy, ga_grouped, ga_raw, 0, HALF)
         bgr = keep.tile([P, F], F32)
         nc.scalar.copy(out=bgr[:], in_=bgr_ps[:])
+        bgo_ps = setup_ps.tile([P, F], F32, tag="setup")
+        nc.tensor.matmul(out=bgo_ps[:], lhsT=ones[:], rhs=bias_rows[:, 2, :], start=True, stop=True)
+        bgo = keep.tile([P, F], F32)
+        nc.scalar.copy(out=bgo[:], in_=bgo_ps[:])
+        regroup(nc.scalar.copy, go_grouped, go_raw)
 
         a_view = a_t[:].rearrange("p t r -> p r t")
 
-        def add_pairs(engine, rel0, a_part, first_j, size, b):
-            shape = [P, size, NODES, PACK]
-            tokens = slice(b * NODES, (b + 1) * NODES)
+        def add_pairs(engine, rel0, a_part, first_j, first_slot, last_slot):
+            count = last_slot - first_slot
+            shape = [P, count, BATCH, NODES, PACK]
             engine.tensor_tensor(
-                out=rel0[:, 0:size, tokens, :],
-                in0=a_part[:, tokens, :].unsqueeze(1).to_broadcast(shape),
-                in1=b_plus[:, b * NODES + first_j : b * NODES + first_j + size, :].unsqueeze(2).to_broadcast(shape),
+                out=rel0[:, first_slot:last_slot, :, :].rearrange("p j (b i) t -> p j b i t", b=BATCH),
+                in0=a_part.rearrange("p (b i) t -> p b i t", b=BATCH).unsqueeze(1).to_broadcast(shape),
+                in1=b_plus[:, first_j + first_slot : first_j + last_slot, :, :].unsqueeze(3).to_broadcast(shape),
                 op=ADD,
             )
 
         def form_rel0(first_j, size):
             rel0 = stream.tile([P, MAX_CHUNK, TOKENS, PACK], BF16, align_bytes=64)
-            for b in range(BATCH):
-                if b < GPSIMD_B:
-                    add_pairs(nc.gpsimd, rel0, a_sb, first_j, size, b)
-                else:
-                    add_pairs(nc.vector, rel0, a_view, first_j, size, b)
+            cut = GPSIMD_TILES[size]
+            if cut > 0:
+                add_pairs(nc.gpsimd, rel0, a_sb[:], first_j, 0, cut)
+            add_pairs(nc.vector, rel0, a_view, first_j, cut, size)
             return rel0
 
         def quantise_rel0(rel0, first_j, size):
@@ -254,51 +275,116 @@ def tile_languagemsgencoder_pa_kernel(
             nc.vector.tensor_tensor(out=result, in0=acc[:], in1=addend[:], op=ADD)
             nc.scalar.activation(out=result, in_=result, func=TANH)
 
+        def flip_products(j):
+            banks = []
+            for half in range(2):
+                bank = setup_ps.tile([P, 2, 2 * TOKENS], F32, tag="setup")
+                for u in range(2):
+                    first = (2 * half + u) * P
+                    out = bank[:, u, :]
+                    mx_pass(nc, out, columns(gb, first, P), columns(xj, j * TOKENS, 2 * TOKENS), start=True, stop=False)
+                    mx_pass(nc, out, columns(ga, first, P), (x2_codes[:], x2_scales[:]), start=False, stop=False)
+                    mx_pass(nc, out, columns(gc, first, P), columns(rel0_mx, j * TOKENS, 2 * TOKENS), start=False, stop=True)
+                banks.append(bank)
+            return banks
+
+        def flip_tanh(bank, half, flipped):
+            for u in range(2):
+                block = 2 * half + u
+                nc.scalar.activation(
+                    out=flipped[:, block, :], in_=bank[:, u, :], func=TANH, bias=bgr_cols[:, block : block + 1]
+                )
+
+        def flip_back(flipped, slot):
+            bank = setup_ps.tile([P, F], F32, tag="setup")
+            for block in range(F // P):
+                nc.tensor.transpose(
+                    bank[:, block * P : (block + 1) * P], flipped[:, block, slot * TOKENS : (slot + 1) * TOKENS], ident[:]
+                )
+            return bank
+
+        def store(result, j):
+            nc.sync.dma_start(out=rel_rows[:, j : j + 2, :], in_=result[:])
+
+        def straight_tiles(chunk):
+            first, size = starts[chunk], CHUNKS[chunk]
+            return list(range(first, first + (2 if chunk in FLIPPED else size)))
+
+        to_open = [j for chunk in range(len(CHUNKS)) for j in straight_tiles(chunk)]
+        accs = {}
+        in_banks = []
+        quantised = [0]
+
+        def open_tiles(limit):
+            while to_open and to_open[0] < limit and len(in_banks) < ACC_BANKS:
+                j = to_open[0]
+                to_open.remove(j)
+                in_banks.append(j)
+                accs[j] = open_tile(j)
+                if j < quantised[0]:
+                    close_tile(accs[j], j)
+
+        def quantise_chunk(rel0, chunk):
+            first, size = starts[chunk], CHUNKS[chunk]
+            quantise_rel0(rel0, first, size)
+            quantised[0] = first + size
+            for j in straight_tiles(chunk):
+                if j in accs:
+                    close_tile(accs[j], j)
+
         rel0 = form_rel0(0, CHUNKS[0])
         gb = quantise_weight(nc, keep, gb_grouped, "gb")
-        accs = {j: open_tile(j) for j in range(CHUNKS[0] + 2)}
+        open_tiles(starts[2])
         gc = quantise_weight(nc, keep, gc_grouped, "gc")
         regroup(nc.vector.tensor_copy, ga_grouped, ga_raw, HALF, F)
         ga = quantise_weight(nc, keep, ga_grouped, "ga")
         c_ps = setup_ps.tile([P, F], F32, tag="setup")
         mx_pass(nc, c_ps[:], x_mx, columns(ga, 0, F), start=True, stop=True)
-        quantise_rel0(rel0, 0, CHUNKS[0])
-        for j in range(CHUNKS[0]):
-            close_tile(accs[j], j)
+        quantise_chunk(rel0, 0)
         c_gr = keep.tile([P, F], F32)
         nc.vector.tensor_tensor(out=c_gr[:], in0=c_ps[:], in1=bgr[:], op=ADD)
 
-        opened, closed = CHUNKS[0] + 2, CHUNKS[0]
-        for chunk in range(1, len(CHUNKS) + 1):
-            first, size = (starts[chunk], CHUNKS[chunk]) if chunk < len(CHUNKS) else (NODES, 0)
-            if chunk < len(CHUNKS):
-                rel0 = form_rel0(first, size)
-            previous = CHUNKS[chunk - 1]
-            result = results.tile([P, MAX_CHUNK, F], F32)
-            for j in range(first - previous, first):
-                finish(accs[j], c_gr, result[:, j - first + previous, :])
-                if opened < first + size:
-                    accs[opened] = open_tile(opened)
-                    opened += 1
-            nc.sync.dma_start(out=rel_rows[:, first - previous : first, :], in_=result[:, 0:previous, :])
-            if chunk + 1 < len(CHUNKS):
-                repeat_xj(first + size, first + size + CHUNKS[chunk + 1])
-            if chunk < len(CHUNKS):
-                quantise_rel0(rel0, first, size)
-            while closed < first + size:
-                close_tile(accs[closed], closed)
-                closed += 1
-            if chunk == 1:
-                regroup(nc.scalar.copy, go_grouped, go_raw)
-            if chunk == 4:
-                go = quantise_weight(nc, keep, go_grouped, "go")
-                bgo_ps = setup_ps.tile([P, F], F32, tag="setup")
-                nc.tensor.matmul(out=bgo_ps[:], lhsT=ones[:], rhs=bias_rows[:, 2, :], start=True, stop=True)
-                bgo = keep.tile([P, F], F32)
-                nc.scalar.copy(out=bgo[:], in_=bgo_ps[:])
-                new_x_acc = setup_ps.tile([P, F], F32, tag="setup")
-                mx_pass(nc, new_x_acc[:], x_mx, columns(go, 0, F), start=True, stop=True)
-            if chunk == 5:
+        products = None
+        flipped = None
+        flipped_j = products_j = 0
+        last = len(CHUNKS)
+        for chunk in range(1, last + 2):
+            backs = [flip_back(flipped, slot) for slot in range(2)] if flipped else []
+            back_j, flipped, products = flipped_j, None, None
+            if chunk - 1 in FLIPPED:
+                products_j = starts[chunk - 1] + 2
+                products = flip_products(products_j)
+            if chunk < last:
+                rel0 = form_rel0(starts[chunk], CHUNKS[chunk])
+            if backs:
+                result = results.tile([P, 2, F], F32, name="result")
+                for slot in range(2):
+                    nc.scalar.copy(out=result[:, slot, :], in_=backs[slot][:])
+                store(result, back_j)
+            if products:
+                flipped, flipped_j = flips.tile([P, F // P, 2 * TOKENS], F32, name="flipped"), products_j
+            if chunk <= last:
+                for n, j in enumerate(straight_tiles(chunk - 1)):
+                    if n % 2 == 0:
+                        result = results.tile([P, 2, F], F32, name="result")
+                    if products:
+                        flip_tanh(products[n], n, flipped)
+                    finish(accs[j], c_gr, result[:, n % 2, :])
+                    in_banks.remove(j)
+                    open_tiles(starts[min(chunk + 1, last - 1)] if chunk + 1 < last else NODES)
+                    if n % 2 == 1:
+                        store(result, j - 1)
+            if chunk == NEW_X_CHUNK + 1:
                 new_x = keep.tile([P, F], F32)
                 finish(new_x_acc, bgo, new_x[:])
+                in_banks.remove(NODES)
                 nc.sync.dma_start(out=out_0.rearrange("b n f -> (b n) f"), in_=new_x[:])
+            if chunk + 1 < last:
+                repeat_xj(starts[chunk + 1], starts[chunk + 1] + CHUNKS[chunk + 1])
+            if chunk < last:
+                quantise_chunk(rel0, chunk)
+            if chunk == NEW_X_CHUNK:
+                go = quantise_weight(nc, keep, go_grouped, "go")
+                new_x_acc = acc_ps.tile([P, F], F32, tag="acc")
+                in_banks.append(NODES)
+                mx_pass(nc, new_x_acc[:], x_mx, columns(go, 0, F), start=True, stop=True)

@@ -27,10 +27,10 @@ BYTES_PER_WORD = 4
 WORDS = NODES // BYTES_PER_WORD
 CHUNKS = [2, 4, 4, 4, 4, 4, 4, 4, 2]
 MAX_CHUNK = max(CHUNKS)
-NEW_X_CHUNK = 5
-FLIPPED = (1, 2, 3, 4, 5, 6)
+NEW_X_CHUNK = 2
+FLIPPED = (0, 1, 3, 5)
 ACC_BANKS = 3
-GPSIMD_TILES = {8: 4, 4: 2, 2: 1}
+GP = [2, 7, 7, 10, 7, 10, 7, 10, 6]
 
 
 FLOPS = 2 * (5 * TOKENS * D * F + PAIRS * D * F)
@@ -90,6 +90,7 @@ def tile_languagemsgencoder_pa_kernel(
     tc, text_embedding, W_rel, b_rel, W_go, b_go, W_gr, b_gr, out_0, out_1
 ):
     nc = tc.nc
+    new_x_rows = out_0.rearrange("b n f -> (b n) f")
     rel_rows = out_1.rearrange("b i j f -> (b i) j f")
 
     with ExitStack() as ctx:
@@ -135,29 +136,35 @@ def tile_languagemsgencoder_pa_kernel(
             nc.tensor.transpose(x_t[:, u, :], x_words[:, u : D // 2 : 2], ident[:])
         rb_grouped = new_grouped(keep, "rb_grouped")
         ra_grouped = new_grouped(keep, "ra_grouped")
-        regroup_by_channel(nc.vector.tensor_copy, rb_grouped, rb_raw, 0, 2)
-        regroup_by_channel(nc.scalar.copy, rb_grouped, rb_raw, 2, 4)
         x_grouped = keep.tile([P, TOKENS, PACK], BF16, align_bytes=64)
-        nc.vector.tensor_copy(
+        nc.scalar.copy(
             out=x_grouped[:].rearrange("p r t -> p (r t)").bitcast(F32).rearrange("p (r u) -> p r u", u=2),
             in_=x_t[:].rearrange("p u r -> p r u"),
         )
-        bias_t = setup_ps.tile([P, 2 * PACK], F32, tag="setup")
+        bias_t = setup_ps.tile([P, 3, PACK], F32, tag="setup")
         for t in range(PACK):
-            for column, row in ((t, bias_rows[:, 0, t:F:PACK]), (PACK + t, bias_rows[:, 1, t * P : (t + 1) * P])):
+            for row, values in enumerate((slice(t, F, PACK), slice(t * P, (t + 1) * P), slice(t * P, (t + 1) * P))):
                 nc.tensor.matmul(
-                    out=bias_t[:, column : column + 1], lhsT=row, rhs=ones[:, 0:1], start=True, stop=True
+                    out=bias_t[:, row, t : t + 1], lhsT=bias_rows[:, row, values], rhs=ones[:, 0:1], start=True, stop=True
                 )
         bgr_ps = setup_ps.tile([P, F], F32, tag="setup")
         nc.tensor.matmul(out=bgr_ps[:], lhsT=ones[:], rhs=bias_rows[:, 1, :], start=True, stop=True)
-        bias_cols = keep.tile([P, 2 * PACK], F32)
-        nc.vector.tensor_copy(out=bias_cols[:], in_=bias_t[:])
-        brel = bias_cols[:, 0:PACK]
-        bgr_cols = bias_cols[:, PACK : 2 * PACK]
+        bias_cols = keep.tile([P, 3, PACK], F32)
+        brel = bias_cols[:, 0, :]
+        bgr_cols = bias_cols[:, 1, :]
+        bgo_cols = bias_cols[:, 2, :]
         nc.vector.quantize_mx(
             out=x_codes[:].bitcast(FP8X4), scales=x_scales[:], in_=x_grouped[:].rearrange("p r t -> p (r t)")
         )
         x_mx = (x_codes[:], x_scales[:])
+        x4_scales = keep.tile([P, TOKENS, BYTES_PER_WORD], U8, align_bytes=64)
+        for c in range(BYTES_PER_WORD):
+            nc.vector.tensor_copy(out=x4_scales[:, :, c], in_=x_scales[:])
+        x4_words = x4_scales[:].rearrange("p r c -> p (r c)").bitcast(I32)
+
+        regroup_by_channel(nc.vector.tensor_copy, rb_grouped, rb_raw, 0, 2)
+        regroup_by_channel(nc.scalar.copy, rb_grouped, rb_raw, 2, 4)
+        nc.vector.tensor_copy(out=bias_cols[:], in_=bias_t[:])
         x2_codes = keep.tile([P, 2 * TOKENS], U32, align_bytes=64)
         x2_scales = keep.tile([P, 2 * TOKENS], U8, align_bytes=64)
 
@@ -167,11 +174,6 @@ def tile_languagemsgencoder_pa_kernel(
         xj_codes = keep.tile([P, PAIRS], U32, align_bytes=64)
         xj_scales = keep.tile([P, PAIRS], U8, align_bytes=64)
         xj = (xj_codes, xj_scales)
-
-        x4_scales = keep.tile([P, TOKENS, BYTES_PER_WORD], U8, align_bytes=64)
-        for c in range(BYTES_PER_WORD):
-            nc.vector.tensor_copy(out=x4_scales[:, :, c], in_=x_scales[:])
-        x4_words = x4_scales[:].rearrange("p r c -> p (r c)").bitcast(I32)
 
         def repeat_xj(first_j, last_j):
             count = last_j - first_j
@@ -229,30 +231,33 @@ def tile_languagemsgencoder_pa_kernel(
         regroup(nc.scalar.copy, ga_grouped, ga_raw, 0, HALF)
         bgr = keep.tile([P, F], F32)
         nc.scalar.copy(out=bgr[:], in_=bgr_ps[:])
-        bgo_ps = setup_ps.tile([P, F], F32, tag="setup")
-        nc.tensor.matmul(out=bgo_ps[:], lhsT=ones[:], rhs=bias_rows[:, 2, :], start=True, stop=True)
-        bgo = keep.tile([P, F], F32)
-        nc.scalar.copy(out=bgo[:], in_=bgo_ps[:])
         regroup(nc.scalar.copy, go_grouped, go_raw)
 
         a_view = a_t[:].rearrange("p t r -> p r t")
 
-        def add_pairs(engine, rel0, a_part, first_j, first_slot, last_slot):
-            count = last_slot - first_slot
-            shape = [P, count, BATCH, NODES, PACK]
-            engine.tensor_tensor(
-                out=rel0[:, first_slot:last_slot, :, :].rearrange("p j (b i) t -> p j b i t", b=BATCH),
-                in0=a_part.rearrange("p (b i) t -> p b i t", b=BATCH).unsqueeze(1).to_broadcast(shape),
-                in1=b_plus[:, first_j + first_slot : first_j + last_slot, :, :].unsqueeze(3).to_broadcast(shape),
-                op=ADD,
-            )
+        def add_pairs(engine, rel0, a_part, first_j, first, last):
+            while first < last:
+                j, b = divmod(first, BATCH)
+                tiles = (last - first) // BATCH if b == 0 else 0
+                items = BATCH if tiles else min(BATCH - b, last - first)
+                tiles = max(tiles, 1)
+                shape = [P, tiles, items, NODES, PACK]
+                engine.tensor_tensor(
+                    out=rel0[:, j : j + tiles, :, :].rearrange("p j (b i) t -> p j b i t", b=BATCH)[:, :, b : b + items, :, :],
+                    in0=a_part.rearrange("p (b i) t -> p b i t", b=BATCH)[:, b : b + items, :, :]
+                    .unsqueeze(1)
+                    .to_broadcast(shape),
+                    in1=b_plus[:, first_j + j : first_j + j + tiles, b : b + items, :].unsqueeze(3).to_broadcast(shape),
+                    op=ADD,
+                )
+                first += tiles * items
 
-        def form_rel0(first_j, size):
+        def form_rel0(chunk):
+            first_j, size = starts[chunk], CHUNKS[chunk]
             rel0 = stream.tile([P, MAX_CHUNK, TOKENS, PACK], BF16, align_bytes=64)
-            cut = GPSIMD_TILES[size]
-            if cut > 0:
-                add_pairs(nc.gpsimd, rel0, a_sb[:], first_j, 0, cut)
-            add_pairs(nc.vector, rel0, a_view, first_j, cut, size)
+            cut = GP[chunk]
+            add_pairs(nc.gpsimd, rel0, a_sb[:], first_j, 0, cut)
+            add_pairs(nc.vector, rel0, a_view, first_j, cut, size * BATCH)
             return rel0
 
         def quantise_rel0(rel0, first_j, size):
@@ -275,24 +280,28 @@ def tile_languagemsgencoder_pa_kernel(
             nc.vector.tensor_tensor(out=result, in0=acc[:], in1=addend[:], op=ADD)
             nc.scalar.activation(out=result, in_=result, func=TANH)
 
-        def flip_products(j):
+        def flip_products(terms, width):
             banks = []
             for half in range(2):
-                bank = setup_ps.tile([P, 2, 2 * TOKENS], F32, tag="setup")
+                bank = setup_ps.tile([P, 2, width], F32, tag="setup")
                 for u in range(2):
-                    first = (2 * half + u) * P
-                    out = bank[:, u, :]
-                    mx_pass(nc, out, columns(gb, first, P), columns(xj, j * TOKENS, 2 * TOKENS), start=True, stop=False)
-                    mx_pass(nc, out, columns(ga, first, P), (x2_codes[:], x2_scales[:]), start=False, stop=False)
-                    mx_pass(nc, out, columns(gc, first, P), columns(rel0_mx, j * TOKENS, 2 * TOKENS), start=False, stop=True)
+                    for n, (weight, moving) in enumerate(terms):
+                        mx_pass(
+                            nc,
+                            bank[:, u, :],
+                            columns(weight, (2 * half + u) * P, P),
+                            moving,
+                            start=n == 0,
+                            stop=n == len(terms) - 1,
+                        )
                 banks.append(bank)
             return banks
 
-        def flip_tanh(bank, half, flipped):
+        def flip_tanh(bank, half, flipped, bias_cols):
             for u in range(2):
                 block = 2 * half + u
                 nc.scalar.activation(
-                    out=flipped[:, block, :], in_=bank[:, u, :], func=TANH, bias=bgr_cols[:, block : block + 1]
+                    out=flipped[:, block, :], in_=bank[:, u, :], func=TANH, bias=bias_cols[:, block : block + 1]
                 )
 
         def flip_back(flipped, slot):
@@ -306,9 +315,19 @@ def tile_languagemsgencoder_pa_kernel(
         def store(result, j):
             nc.sync.dma_start(out=rel_rows[:, j : j + 2, :], in_=result[:])
 
+        def flip_of(chunk):
+            if chunk in FLIPPED:
+                j = starts[chunk] + CHUNKS[chunk] - 2
+                x2 = (x2_codes[:], x2_scales[:])
+                terms = [(gb, columns(xj, j * TOKENS, 2 * TOKENS)), (ga, x2), (gc, columns(rel0_mx, j * TOKENS, 2 * TOKENS))]
+                return terms, 2, bgr_cols, rel_rows[:, j : j + 2, :]
+            if chunk == NEW_X_CHUNK:
+                return [(go, x_mx)], 1, bgo_cols, new_x_rows
+            return None
+
         def straight_tiles(chunk):
             first, size = starts[chunk], CHUNKS[chunk]
-            return list(range(first, first + (2 if chunk in FLIPPED else size)))
+            return list(range(first, first + (size - 2 if chunk in FLIPPED else size)))
 
         to_open = [j for chunk in range(len(CHUNKS)) for j in straight_tiles(chunk)]
         accs = {}
@@ -332,7 +351,7 @@ def tile_languagemsgencoder_pa_kernel(
                 if j in accs:
                     close_tile(accs[j], j)
 
-        rel0 = form_rel0(0, CHUNKS[0])
+        rel0 = form_rel0(0)
         gb = quantise_weight(nc, keep, gb_grouped, "gb")
         open_tiles(starts[2])
         gc = quantise_weight(nc, keep, gc_grouped, "gc")
@@ -344,47 +363,49 @@ def tile_languagemsgencoder_pa_kernel(
         c_gr = keep.tile([P, F], F32)
         nc.vector.tensor_tensor(out=c_gr[:], in0=c_ps[:], in1=bgr[:], op=ADD)
 
-        products = None
         flipped = None
-        flipped_j = products_j = 0
         last = len(CHUNKS)
         for chunk in range(1, last + 2):
-            backs = [flip_back(flipped, slot) for slot in range(2)] if flipped else []
-            back_j, flipped, products = flipped_j, None, None
-            if chunk - 1 in FLIPPED:
-                products_j = starts[chunk - 1] + 2
-                products = flip_products(products_j)
+            backs = []
+            if flipped:
+                backs = [flip_back(flipped, slot) for slot in range(back_tiles)]
+                back_rows = flip_rows
+            flip = flip_of(chunk - 1)
+            flipped = None
+            if flip:
+                terms, back_tiles, bias, flip_rows = flip
+                products = flip_products(terms, back_tiles * TOKENS)
             if chunk < last:
-                rel0 = form_rel0(starts[chunk], CHUNKS[chunk])
+                rel0 = form_rel0(chunk)
             if backs:
                 result = results.tile([P, 2, F], F32, name="result")
-                for slot in range(2):
-                    nc.scalar.copy(out=result[:, slot, :], in_=backs[slot][:])
-                store(result, back_j)
-            if products:
-                flipped, flipped_j = flips.tile([P, F // P, 2 * TOKENS], F32, name="flipped"), products_j
-            if chunk <= last:
-                for n, j in enumerate(straight_tiles(chunk - 1)):
+                for slot, back in enumerate(backs):
+                    nc.scalar.copy(out=result[:, slot, :], in_=back[:])
+                if len(backs) == 1:
+                    nc.sync.dma_start(out=back_rows, in_=result[:, 0, :])
+                else:
+                    nc.sync.dma_start(out=back_rows, in_=result[:])
+            straight = straight_tiles(chunk - 1) if chunk <= last else []
+            if flip:
+                flipped = flips.tile([P, F // P, 2 * TOKENS], F32, name="flipped")
+                flipped = flipped[:, :, 0 : back_tiles * TOKENS]
+            for n in range(max(len(straight), 2)):
+                if flip and n < 2:
+                    flip_tanh(products[n], n, flipped, bias)
+                if n < len(straight):
+                    j = straight[n]
                     if n % 2 == 0:
                         result = results.tile([P, 2, F], F32, name="result")
-                    if products:
-                        flip_tanh(products[n], n, flipped)
                     finish(accs[j], c_gr, result[:, n % 2, :])
                     in_banks.remove(j)
-                    open_tiles(starts[min(chunk + 1, last - 1)] if chunk + 1 < last else NODES)
-                    if n % 2 == 1:
+                    open_tiles(starts[chunk + 1] if chunk + 1 < last else NODES)
+                    if chunk == last:
+                        nc.sync.dma_start(out=rel_rows[:, j, :], in_=result[:, n % 2, :])
+                    elif n % 2 == 1:
                         store(result, j - 1)
-            if chunk == NEW_X_CHUNK + 1:
-                new_x = keep.tile([P, F], F32)
-                finish(new_x_acc, bgo, new_x[:])
-                in_banks.remove(NODES)
-                nc.sync.dma_start(out=out_0.rearrange("b n f -> (b n) f"), in_=new_x[:])
-            if chunk + 1 < last:
-                repeat_xj(starts[chunk + 1], starts[chunk + 1] + CHUNKS[chunk + 1])
             if chunk < last:
                 quantise_chunk(rel0, chunk)
+            if chunk + 1 < last:
+                repeat_xj(starts[chunk + 1], starts[chunk + 1] + CHUNKS[chunk + 1])
             if chunk == NEW_X_CHUNK:
                 go = quantise_weight(nc, keep, go_grouped, "go")
-                new_x_acc = acc_ps.tile([P, F], F32, tag="acc")
-                in_banks.append(NODES)
-                mx_pass(nc, new_x_acc[:], x_mx, columns(go, 0, F), start=True, stop=True)

@@ -11,6 +11,7 @@ U8 = mybir.dt.uint8
 FP8X4 = mybir.dt.float8_e4m3fn_x4
 ADD = mybir.AluOpType.add
 TANH = mybir.ActivationFunctionType.Tanh
+IDENTITY = mybir.ActivationFunctionType.Identity
 
 P = 128
 PACK = 4
@@ -25,12 +26,14 @@ HALF = F // 2
 
 BYTES_PER_WORD = 4
 WORDS = NODES // BYTES_PER_WORD
-CHUNKS = [2, 4, 4, 4, 4, 4, 4, 4, 2]
+CHUNKS = [4] * 8
 MAX_CHUNK = max(CHUNKS)
-NEW_X_CHUNK = 2
-FLIPPED = (0, 1, 3, 5)
+GA_CUT = F // 2
+NEW_X_CHUNK = 5
+GO_CHUNK = 3
+FLIPPED = (0, 2, 4)
 ACC_BANKS = 3
-GP = [2, 7, 7, 10, 7, 10, 7, 10, 6]
+GP = [4, 7, 10, 7, 10, 7, 10, 10]
 
 
 FLOPS = 2 * (5 * TOKENS * D * F + PAIRS * D * F)
@@ -51,6 +54,19 @@ def regroup(copy, grouped, raw, first=0, last=F):
         out=grouped[:, first:last, :].rearrange("p (c i) t -> p c t i", i=4),
         in_=raw[:, :, first:last].rearrange("p t (c i) -> p c t i", i=4),
     )
+
+
+def regroup_in_psum(nc, pool, ident, raw):
+    bank = pool.tile([P, HALF, PACK], BF16, tag="setup")
+    for first in (0, P):
+        nc.tensor.matmul(
+            out=bank[:, first : first + P, :],
+            lhsT=ident,
+            rhs=raw[:, :, first : first + P].rearrange("p t n -> p n t"),
+            start=True,
+            stop=True,
+        )
+    return bank
 
 
 def regroup_by_channel(copy, grouped, raw, first, last):
@@ -114,6 +130,8 @@ def tile_languagemsgencoder_pa_kernel(
         nc.vector.memset(bias_rows[:].rearrange("p a f -> p (a f)").bitcast(I32), 0)
         ones = keep.tile([P, P], BF16)
         nc.vector.memset(ones[:], 1.0)
+        ident_bf = keep.tile([P, P], BF16)
+        nc.vector.tensor_copy(out=ident_bf[:], in_=ident[:])
 
         x_sb = keep.tile([P, D], BF16)
         nc.sync.dma_start(out=x_sb[:], in_=text_embedding.rearrange("b n d -> (b n) d"))
@@ -147,8 +165,6 @@ def tile_languagemsgencoder_pa_kernel(
                 nc.tensor.matmul(
                     out=bias_t[:, row, t : t + 1], lhsT=bias_rows[:, row, values], rhs=ones[:, 0:1], start=True, stop=True
                 )
-        bgr_ps = setup_ps.tile([P, F], F32, tag="setup")
-        nc.tensor.matmul(out=bgr_ps[:], lhsT=ones[:], rhs=bias_rows[:, 1, :], start=True, stop=True)
         bias_cols = keep.tile([P, 3, PACK], F32)
         brel = bias_cols[:, 0, :]
         bgr_cols = bias_cols[:, 1, :]
@@ -213,7 +229,7 @@ def tile_languagemsgencoder_pa_kernel(
         regroup(nc.scalar.copy, gc_grouped, gc_raw, 0, HALF)
         starts = [sum(CHUNKS[:c]) for c in range(len(CHUNKS))]
         repeat_xj(0, starts[2])
-        regroup(nc.vector.tensor_copy, gb_grouped, gb_raw)
+        regroup(nc.vector.tensor_copy, gb_grouped, gb_raw, HALF, F)
         nc.vector.tensor_copy(
             out=x2_codes[:].bitcast(I32).rearrange("p (e r) -> p e r", e=2),
             in_=x_codes[:].bitcast(I32).unsqueeze(1).to_broadcast([P, 2, TOKENS]),
@@ -225,13 +241,12 @@ def tile_languagemsgencoder_pa_kernel(
         a_t = keep_ps.tile([P, PACK, TOKENS], F32)
         for t in range(PACK):
             mx_pass(nc, a_t[:, t, :], columns(ra, t * P, P), x_mx, start=True, stop=True)
+        gb_bank = regroup_in_psum(nc, setup_ps, ident_bf[:], gb_raw)
         a_sb = keep.tile([P, TOKENS, PACK], F32)
         nc.scalar.copy(out=a_sb[:], in_=a_t[:].rearrange("p t r -> p r t"))
         regroup(nc.scalar.copy, gc_grouped, gc_raw, HALF, F)
-        regroup(nc.scalar.copy, ga_grouped, ga_raw, 0, HALF)
-        bgr = keep.tile([P, F], F32)
-        nc.scalar.copy(out=bgr[:], in_=bgr_ps[:])
-        regroup(nc.scalar.copy, go_grouped, go_raw)
+        nc.scalar.copy(out=gb_grouped[:, 0:HALF, :], in_=gb_bank[:])
+        regroup(nc.scalar.copy, ga_grouped, ga_raw, 0, GA_CUT)
 
         a_view = a_t[:].rearrange("p t r -> p r t")
 
@@ -281,27 +296,28 @@ def tile_languagemsgencoder_pa_kernel(
             nc.scalar.activation(out=result, in_=result, func=TANH)
 
         def flip_products(terms, width):
+            blocks = F // width
             banks = []
-            for half in range(2):
-                bank = setup_ps.tile([P, 2, width], F32, tag="setup")
-                for u in range(2):
-                    for n, (weight, moving) in enumerate(terms):
-                        mx_pass(
-                            nc,
-                            bank[:, u, :],
-                            columns(weight, (2 * half + u) * P, P),
-                            moving,
-                            start=n == 0,
-                            stop=n == len(terms) - 1,
-                        )
-                banks.append(bank)
+            for block in range(F // P):
+                if block % blocks == 0:
+                    bank = setup_ps.tile([P, blocks, width], F32, tag="setup")
+                    banks.append(bank)
+                for n, (weight, moving) in enumerate(terms):
+                    mx_pass(
+                        nc,
+                        banks[-1][:, block % blocks, :],
+                        columns(weight, block * P, P),
+                        moving,
+                        start=n == 0,
+                        stop=n == len(terms) - 1,
+                    )
             return banks
 
-        def flip_tanh(bank, half, flipped, bias_cols):
-            for u in range(2):
-                block = 2 * half + u
+        def flip_out(bank, first, flipped, func, bias_cols):
+            for u in range(bank.shape[1]):
+                block = first + u
                 nc.scalar.activation(
-                    out=flipped[:, block, :], in_=bank[:, u, :], func=TANH, bias=bias_cols[:, block : block + 1]
+                    out=flipped[:, block, :], in_=bank[:, u, :], func=func, bias=bias_cols[:, block : block + 1]
                 )
 
         def flip_back(flipped, slot):
@@ -352,16 +368,19 @@ def tile_languagemsgencoder_pa_kernel(
                     close_tile(accs[j], j)
 
         rel0 = form_rel0(0)
+        regroup(nc.vector.tensor_copy, ga_grouped, ga_raw, GA_CUT, F)
+        ga = quantise_weight(nc, keep, ga_grouped, "ga")
+        c_flipped = keep.tile([P, F // P, TOKENS], F32)
+        (c_bank,) = flip_products([(ga, x_mx)], TOKENS)
+        regroup(nc.scalar.copy, go_grouped, go_raw, 0, HALF)
+        flip_out(c_bank, 0, c_flipped[:], IDENTITY, bgr_cols)
         gb = quantise_weight(nc, keep, gb_grouped, "gb")
         open_tiles(starts[2])
-        gc = quantise_weight(nc, keep, gc_grouped, "gc")
-        regroup(nc.vector.tensor_copy, ga_grouped, ga_raw, HALF, F)
-        ga = quantise_weight(nc, keep, ga_grouped, "ga")
-        c_ps = setup_ps.tile([P, F], F32, tag="setup")
-        mx_pass(nc, c_ps[:], x_mx, columns(ga, 0, F), start=True, stop=True)
-        quantise_chunk(rel0, 0)
+        c_back = flip_back(c_flipped[:], 0)
         c_gr = keep.tile([P, F], F32)
-        nc.vector.tensor_tensor(out=c_gr[:], in0=c_ps[:], in1=bgr[:], op=ADD)
+        nc.scalar.copy(out=c_gr[:], in_=c_back[:])
+        gc = quantise_weight(nc, keep, gc_grouped, "gc")
+        quantise_chunk(rel0, 0)
 
         flipped = None
         last = len(CHUNKS)
@@ -390,8 +409,8 @@ def tile_languagemsgencoder_pa_kernel(
                 flipped = flips.tile([P, F // P, 2 * TOKENS], F32, name="flipped")
                 flipped = flipped[:, :, 0 : back_tiles * TOKENS]
             for n in range(max(len(straight), 2)):
-                if flip and n < 2:
-                    flip_tanh(products[n], n, flipped, bias)
+                if flip and n < len(products):
+                    flip_out(products[n], n * (F // P) // len(products), flipped, TANH, bias)
                 if n < len(straight):
                     j = straight[n]
                     if n % 2 == 0:
@@ -407,5 +426,7 @@ def tile_languagemsgencoder_pa_kernel(
                 quantise_chunk(rel0, chunk)
             if chunk + 1 < last:
                 repeat_xj(starts[chunk + 1], starts[chunk + 1] + CHUNKS[chunk + 1])
+            if chunk == GO_CHUNK:
+                regroup(nc.scalar.copy, go_grouped, go_raw, HALF, F)
             if chunk == NEW_X_CHUNK:
                 go = quantise_weight(nc, keep, go_grouped, "go")

@@ -23,6 +23,7 @@ F = 512
 PAIRS = BATCH * NODES * NODES
 
 HALF = F // 2
+HALVES = (slice(0, HALF), slice(HALF, F))
 
 BYTES_PER_WORD = 4
 WORDS = NODES // BYTES_PER_WORD
@@ -54,19 +55,6 @@ def regroup(copy, grouped, raw, first=0, last=F):
         out=grouped[:, first:last, :].rearrange("p (c i) t -> p c t i", i=4),
         in_=raw[:, :, first:last].rearrange("p t (c i) -> p c t i", i=4),
     )
-
-
-def regroup_in_psum(nc, pool, ident, raw):
-    bank = pool.tile([P, HALF, PACK], BF16, tag="setup")
-    for first in (0, P):
-        nc.tensor.matmul(
-            out=bank[:, first : first + P, :],
-            lhsT=ident,
-            rhs=raw[:, :, first : first + P].rearrange("p t n -> p n t"),
-            start=True,
-            stop=True,
-        )
-    return bank
 
 
 def regroup_by_channel(copy, grouped, raw, first, last):
@@ -130,8 +118,6 @@ def tile_languagemsgencoder_pa_kernel(
         nc.vector.memset(bias_rows[:].rearrange("p a f -> p (a f)").bitcast(I32), 0)
         ones = keep.tile([P, P], BF16)
         nc.vector.memset(ones[:], 1.0)
-        ident_bf = keep.tile([P, P], BF16)
-        nc.vector.tensor_copy(out=ident_bf[:], in_=ident[:])
 
         x_sb = keep.tile([P, D], BF16)
         nc.sync.dma_start(out=x_sb[:], in_=text_embedding.rearrange("b n d -> (b n) d"))
@@ -229,7 +215,7 @@ def tile_languagemsgencoder_pa_kernel(
         regroup(nc.scalar.copy, gc_grouped, gc_raw, 0, HALF)
         starts = [sum(CHUNKS[:c]) for c in range(len(CHUNKS))]
         repeat_xj(0, starts[2])
-        regroup(nc.vector.tensor_copy, gb_grouped, gb_raw, HALF, F)
+        regroup(nc.vector.tensor_copy, gb_grouped, gb_raw)
         nc.vector.tensor_copy(
             out=x2_codes[:].bitcast(I32).rearrange("p (e r) -> p e r", e=2),
             in_=x_codes[:].bitcast(I32).unsqueeze(1).to_broadcast([P, 2, TOKENS]),
@@ -241,11 +227,9 @@ def tile_languagemsgencoder_pa_kernel(
         a_t = keep_ps.tile([P, PACK, TOKENS], F32)
         for t in range(PACK):
             mx_pass(nc, a_t[:, t, :], columns(ra, t * P, P), x_mx, start=True, stop=True)
-        gb_bank = regroup_in_psum(nc, setup_ps, ident_bf[:], gb_raw)
         a_sb = keep.tile([P, TOKENS, PACK], F32)
         nc.scalar.copy(out=a_sb[:], in_=a_t[:].rearrange("p t r -> p r t"))
         regroup(nc.scalar.copy, gc_grouped, gc_raw, HALF, F)
-        nc.scalar.copy(out=gb_grouped[:, 0:HALF, :], in_=gb_bank[:])
         regroup(nc.scalar.copy, ga_grouped, ga_raw, 0, GA_CUT)
 
         a_view = a_t[:].rearrange("p t r -> p r t")
@@ -275,12 +259,12 @@ def tile_languagemsgencoder_pa_kernel(
             add_pairs(nc.vector, rel0, a_view, first_j, cut, size * BATCH)
             return rel0
 
-        def quantise_rel0(rel0, first_j, size):
-            codes, scales = columns(rel0_mx, first_j * TOKENS, size * TOKENS)
+        def quantise_rel0(rel0, first_j, first_slot, last_slot):
+            codes, scales = columns(rel0_mx, (first_j + first_slot) * TOKENS, (last_slot - first_slot) * TOKENS)
             nc.vector.quantize_mx(
                 out=codes.bitcast(FP8X4),
                 scales=scales,
-                in_=rel0[:, 0:size, :, :].rearrange("p s r t -> p (s r t)"),
+                in_=rel0[:, first_slot:last_slot, :, :].rearrange("p s r t -> p (s r t)"),
             )
 
         def open_tile(j):
@@ -292,7 +276,7 @@ def tile_languagemsgencoder_pa_kernel(
             mx_pass(nc, acc[:], columns(rel0_mx, j * TOKENS, TOKENS), columns(gc, 0, F), start=False, stop=True)
 
         def finish(acc, addend, result):
-            nc.vector.tensor_tensor(out=result, in0=acc[:], in1=addend[:], op=ADD)
+            nc.vector.tensor_tensor(out=result, in0=acc, in1=addend, op=ADD)
             nc.scalar.activation(out=result, in_=result, func=TANH)
 
         def flip_products(terms, width):
@@ -328,17 +312,14 @@ def tile_languagemsgencoder_pa_kernel(
                 )
             return bank
 
-        def store(result, j):
-            nc.sync.dma_start(out=rel_rows[:, j : j + 2, :], in_=result[:])
-
         def flip_of(chunk):
             if chunk in FLIPPED:
                 j = starts[chunk] + CHUNKS[chunk] - 2
                 x2 = (x2_codes[:], x2_scales[:])
                 terms = [(gb, columns(xj, j * TOKENS, 2 * TOKENS)), (ga, x2), (gc, columns(rel0_mx, j * TOKENS, 2 * TOKENS))]
-                return terms, 2, bgr_cols, rel_rows[:, j : j + 2, :]
+                return terms, 2, bgr_cols, [rel_rows[:, j, :], rel_rows[:, j + 1, :]]
             if chunk == NEW_X_CHUNK:
-                return [(go, x_mx)], 1, bgo_cols, new_x_rows
+                return [(go, x_mx)], 1, bgo_cols, [new_x_rows]
             return None
 
         def straight_tiles(chunk):
@@ -361,11 +342,13 @@ def tile_languagemsgencoder_pa_kernel(
 
         def quantise_chunk(rel0, chunk):
             first, size = starts[chunk], CHUNKS[chunk]
-            quantise_rel0(rel0, first, size)
-            quantised[0] = first + size
-            for j in straight_tiles(chunk):
-                if j in accs:
-                    close_tile(accs[j], j)
+            step = size // 2 if chunk == len(CHUNKS) - 1 else size
+            for slot in range(0, size, step):
+                quantise_rel0(rel0, first, slot, slot + step)
+                quantised[0] = first + slot + step
+                for j in straight_tiles(chunk):
+                    if j in accs and first + slot <= j < quantised[0]:
+                        close_tile(accs[j], j)
 
         rel0 = form_rel0(0)
         regroup(nc.vector.tensor_copy, ga_grouped, ga_raw, GA_CUT, F)
@@ -400,10 +383,7 @@ def tile_languagemsgencoder_pa_kernel(
                 result = results.tile([P, 2, F], F32, name="result")
                 for slot, back in enumerate(backs):
                     nc.scalar.copy(out=result[:, slot, :], in_=back[:])
-                if len(backs) == 1:
-                    nc.sync.dma_start(out=back_rows, in_=result[:, 0, :])
-                else:
-                    nc.sync.dma_start(out=back_rows, in_=result[:])
+                    nc.sync.dma_start(out=back_rows[slot], in_=result[:, slot, :])
             straight = straight_tiles(chunk - 1) if chunk <= last else []
             if flip:
                 flipped = flips.tile([P, F // P, 2 * TOKENS], F32, name="flipped")
@@ -415,13 +395,11 @@ def tile_languagemsgencoder_pa_kernel(
                     j = straight[n]
                     if n % 2 == 0:
                         result = results.tile([P, 2, F], F32, name="result")
-                    finish(accs[j], c_gr, result[:, n % 2, :])
+                    for columns_of_f in HALVES if chunk == last else (slice(0, F),):
+                        finish(accs[j][:, columns_of_f], c_gr[:, columns_of_f], result[:, n % 2, columns_of_f])
+                        nc.sync.dma_start(out=rel_rows[:, j, columns_of_f], in_=result[:, n % 2, columns_of_f])
                     in_banks.remove(j)
                     open_tiles(starts[chunk + 1] if chunk + 1 < last else NODES)
-                    if chunk == last:
-                        nc.sync.dma_start(out=rel_rows[:, j, :], in_=result[:, n % 2, :])
-                    elif n % 2 == 1:
-                        store(result, j - 1)
             if chunk < last:
                 quantise_chunk(rel0, chunk)
             if chunk + 1 < last:

@@ -30,6 +30,7 @@ WORDS = NODES // BYTES_PER_WORD
 CHUNKS = [4] * 8
 MAX_CHUNK = max(CHUNKS)
 GA_CUT = F // 2
+WARM_UP_PASSES = 12
 NEW_X_CHUNK = 5
 GO_CHUNK = 3
 FLIPPED = (0, 2, 4)
@@ -194,6 +195,11 @@ def tile_languagemsgencoder_pa_kernel(
                 .to_broadcast([P, count, BATCH, WORDS]),
             )
 
+        def warm_up(count):
+            idle = setup_ps.tile([P, F], F32, tag="setup")
+            for n in range(count):
+                mx_pass(nc, idle[:], x_mx, columns(rb, 0, F), start=True, stop=True)
+
         rb = quantise_weight(nc, keep, rb_grouped, "rb")
         b_t = setup_ps.tile([P, PACK, TOKENS], F32, tag="setup")
         for t in range(PACK):
@@ -227,6 +233,7 @@ def tile_languagemsgencoder_pa_kernel(
         a_t = keep_ps.tile([P, PACK, TOKENS], F32)
         for t in range(PACK):
             mx_pass(nc, a_t[:, t, :], columns(ra, t * P, P), x_mx, start=True, stop=True)
+        warm_up(WARM_UP_PASSES)
         a_sb = keep.tile([P, TOKENS, PACK], F32)
         nc.scalar.copy(out=a_sb[:], in_=a_t[:].rearrange("p t r -> p r t"))
         regroup(nc.scalar.copy, gc_grouped, gc_raw, HALF, F)
@@ -395,11 +402,14 @@ def tile_languagemsgencoder_pa_kernel(
                     j = straight[n]
                     if n % 2 == 0:
                         result = results.tile([P, 2, F], F32, name="result")
-                    for columns_of_f in HALVES if chunk == last else (slice(0, F),):
-                        finish(accs[j][:, columns_of_f], c_gr[:, columns_of_f], result[:, n % 2, columns_of_f])
-                        nc.sync.dma_start(out=rel_rows[:, j, columns_of_f], in_=result[:, n % 2, columns_of_f])
+                    for part in HALVES if chunk == last else (slice(0, F),):
+                        finish(accs[j][:, part], c_gr[:, part], result[:, n % 2, part])
                     in_banks.remove(j)
                     open_tiles(starts[chunk + 1] if chunk + 1 < last else NODES)
+                    if chunk >= last - 1:
+                        nc.sync.dma_start(out=rel_rows[:, j, :], in_=result[:, n % 2, :])
+                    elif n % 2 == 1:
+                        nc.sync.dma_start(out=rel_rows[:, j - 1 : j + 1, :], in_=result[:])
             if chunk < last:
                 quantise_chunk(rel0, chunk)
             if chunk + 1 < last:

@@ -29,13 +29,14 @@ BYTES_PER_WORD = 4
 WORDS = NODES // BYTES_PER_WORD
 CHUNKS = [4] * 8
 MAX_CHUNK = max(CHUNKS)
-GA_CUT = F // 2
+GA_CUT = 3 * P
+M_CUT = P // 2
 WARM_UP_PASSES = 12
 NEW_X_CHUNK = 5
 GO_CHUNK = 3
 FLIPPED = (0, 2, 4)
 ACC_BANKS = 3
-GP = [4, 7, 10, 7, 10, 7, 10, 10]
+GP = [8, 16, 20, 16, 20, 16, 20, 20]
 
 
 FLOPS = 2 * (5 * TOKENS * D * F + PAIRS * D * F)
@@ -60,8 +61,8 @@ def regroup(copy, grouped, raw, first=0, last=F):
 
 def regroup_by_channel(copy, grouped, raw, first, last):
     copy(
-        out=grouped[:].rearrange("p (t m) j -> p t m j", t=PACK)[:, first:last, :, :],
-        in_=raw[:].rearrange("p j (m t) -> p t m j", t=PACK)[:, first:last, :, :],
+        out=grouped[:].rearrange("p (t m) j -> p m j t", t=PACK)[:, first:last, :, :],
+        in_=raw[:].rearrange("p j (m t) -> p m j t", t=PACK)[:, first:last, :, :],
     )
 
 
@@ -165,8 +166,8 @@ def tile_languagemsgencoder_pa_kernel(
             nc.vector.tensor_copy(out=x4_scales[:, :, c], in_=x_scales[:])
         x4_words = x4_scales[:].rearrange("p r c -> p (r c)").bitcast(I32)
 
-        regroup_by_channel(nc.vector.tensor_copy, rb_grouped, rb_raw, 0, 2)
-        regroup_by_channel(nc.scalar.copy, rb_grouped, rb_raw, 2, 4)
+        regroup_by_channel(nc.vector.tensor_copy, rb_grouped, rb_raw, 0, M_CUT)
+        regroup_by_channel(nc.scalar.copy, rb_grouped, rb_raw, M_CUT, P)
         nc.vector.tensor_copy(out=bias_cols[:], in_=bias_t[:])
         x2_codes = keep.tile([P, 2 * TOKENS], U32, align_bytes=64)
         x2_scales = keep.tile([P, 2 * TOKENS], U8, align_bytes=64)
@@ -204,8 +205,8 @@ def tile_languagemsgencoder_pa_kernel(
         b_t = setup_ps.tile([P, PACK, TOKENS], F32, tag="setup")
         for t in range(PACK):
             mx_pass(nc, b_t[:, t, :], columns(rb, t * P, P), x_mx, start=True, stop=True)
-        regroup_by_channel(nc.vector.tensor_copy, ra_grouped, ra_raw, 0, 2)
-        regroup_by_channel(nc.scalar.copy, ra_grouped, ra_raw, 2, 4)
+        regroup_by_channel(nc.vector.tensor_copy, ra_grouped, ra_raw, 0, M_CUT)
+        regroup_by_channel(nc.scalar.copy, ra_grouped, ra_raw, M_CUT, P)
         ra = quantise_weight(nc, keep, ra_grouped, "ra")
         gc_grouped = new_grouped(keep, "gc_grouped")
         gb_grouped = new_grouped(keep, "gb_grouped")
@@ -241,29 +242,34 @@ def tile_languagemsgencoder_pa_kernel(
 
         a_view = a_t[:].rearrange("p t r -> p r t")
 
-        def add_pairs(engine, rel0, a_part, first_j, first, last):
-            while first < last:
-                j, b = divmod(first, BATCH)
-                tiles = (last - first) // BATCH if b == 0 else 0
-                items = BATCH if tiles else min(BATCH - b, last - first)
-                tiles = max(tiles, 1)
-                shape = [P, tiles, items, NODES, PACK]
-                engine.tensor_tensor(
-                    out=rel0[:, j : j + tiles, :, :].rearrange("p j (b i) t -> p j b i t", b=BATCH)[:, :, b : b + items, :, :],
-                    in0=a_part.rearrange("p (b i) t -> p b i t", b=BATCH)[:, b : b + items, :, :]
-                    .unsqueeze(1)
-                    .to_broadcast(shape),
-                    in1=b_plus[:, first_j + j : first_j + j + tiles, b : b + items, :].unsqueeze(3).to_broadcast(shape),
-                    op=ADD,
-                )
-                first += tiles * items
+        def add_pairs(engine, rel0, a_part, first_j, size, first_i, last_i):
+            shape = [P, size, BATCH, last_i - first_i, PACK]
+            engine.tensor_tensor(
+                out=rel0[:, 0:size, :, :].rearrange("p j (b i) t -> p j b i t", b=BATCH)[:, :, :, first_i:last_i, :],
+                in0=a_part.rearrange("p (b i) t -> p b i t", b=BATCH)[:, :, first_i:last_i, :]
+                .unsqueeze(1)
+                .to_broadcast(shape),
+                in1=b_plus[:, first_j : first_j + size, :, :].unsqueeze(3).to_broadcast(shape),
+                op=ADD,
+            )
+
+        def add_item(engine, rel0, a_part, first_j, size, b, first_i):
+            shape = [P, size, NODES - first_i, PACK]
+            tokens = slice(b * NODES + first_i, (b + 1) * NODES)
+            engine.tensor_tensor(
+                out=rel0[:, 0:size, tokens, :],
+                in0=a_part[:, tokens, :].unsqueeze(1).to_broadcast(shape),
+                in1=b_plus[:, first_j : first_j + size, b, :].unsqueeze(2).to_broadcast(shape),
+                op=ADD,
+            )
 
         def form_rel0(chunk):
             first_j, size = starts[chunk], CHUNKS[chunk]
             rel0 = stream.tile([P, MAX_CHUNK, TOKENS, PACK], BF16, align_bytes=64)
             cut = GP[chunk]
-            add_pairs(nc.gpsimd, rel0, a_sb[:], first_j, 0, cut)
-            add_pairs(nc.vector, rel0, a_view, first_j, cut, size * BATCH)
+            add_pairs(nc.gpsimd, rel0, a_sb[:], first_j, size, 0, cut)
+            for b in range(BATCH):
+                add_item(nc.vector, rel0, a_view, first_j, size, b, cut)
             return rel0
 
         def quantise_rel0(rel0, first_j, first_slot, last_slot):

@@ -29,14 +29,15 @@ BYTES_PER_WORD = 4
 WORDS = NODES // BYTES_PER_WORD
 CHUNKS = [4] * 8
 MAX_CHUNK = max(CHUNKS)
-GA_CUT = 3 * P
+GA_CUT = F - P // 2
 M_CUT = P // 2
+GC_CUT = 3 * P
 WARM_UP_PASSES = 12
 NEW_X_CHUNK = 5
 GO_CHUNK = 3
 FLIPPED = (0, 2, 4)
 ACC_BANKS = 3
-GP = [8, 16, 20, 16, 20, 16, 20, 20]
+GPSIMD_I = 20
 
 
 FLOPS = 2 * (5 * TOKENS * D * F + PAIRS * D * F)
@@ -102,7 +103,7 @@ def tile_languagemsgencoder_pa_kernel(
     with ExitStack() as ctx:
         keep = ctx.enter_context(tc.tile_pool(name="keep", bufs=1))
         stream = ctx.enter_context(tc.tile_pool(name="stream", bufs=1))
-        results = ctx.enter_context(tc.tile_pool(name="results", bufs=6))
+        results = ctx.enter_context(tc.tile_pool(name="results", bufs=8))
         flips = ctx.enter_context(tc.tile_pool(name="flips", bufs=2))
         keep_ps = ctx.enter_context(tc.psum_pool(name="keep_ps", bufs=1))
         setup_ps = ctx.enter_context(tc.psum_pool(name="setup_ps", bufs=4))
@@ -219,57 +220,41 @@ def tile_languagemsgencoder_pa_kernel(
             in1=brel.unsqueeze(1).unsqueeze(1).to_broadcast([P, BATCH, NODES, PACK]),
             op=ADD,
         )
-        regroup(nc.scalar.copy, gc_grouped, gc_raw, 0, HALF)
+        regroup(nc.scalar.copy, gc_grouped, gc_raw, 0, GC_CUT)
         starts = [sum(CHUNKS[:c]) for c in range(len(CHUNKS))]
         repeat_xj(0, starts[2])
         regroup(nc.vector.tensor_copy, gb_grouped, gb_raw)
-        nc.vector.tensor_copy(
-            out=x2_codes[:].bitcast(I32).rearrange("p (e r) -> p e r", e=2),
-            in_=x_codes[:].bitcast(I32).unsqueeze(1).to_broadcast([P, 2, TOKENS]),
-        )
-        nc.vector.tensor_copy(
-            out=x2_scales[:].bitcast(I32).rearrange("p (e r) -> p e r", e=2),
-            in_=x_scales[:].bitcast(I32).unsqueeze(1).to_broadcast([P, 2, TOKENS // BYTES_PER_WORD]),
-        )
         a_t = keep_ps.tile([P, PACK, TOKENS], F32)
         for t in range(PACK):
             mx_pass(nc, a_t[:, t, :], columns(ra, t * P, P), x_mx, start=True, stop=True)
         warm_up(WARM_UP_PASSES)
         a_sb = keep.tile([P, TOKENS, PACK], F32)
         nc.scalar.copy(out=a_sb[:], in_=a_t[:].rearrange("p t r -> p r t"))
-        regroup(nc.scalar.copy, gc_grouped, gc_raw, HALF, F)
+        regroup(nc.scalar.copy, gc_grouped, gc_raw, GC_CUT, F)
         regroup(nc.scalar.copy, ga_grouped, ga_raw, 0, GA_CUT)
 
         a_view = a_t[:].rearrange("p t r -> p r t")
 
-        def add_pairs(engine, rel0, a_part, first_j, size, first_i, last_i):
-            shape = [P, size, BATCH, last_i - first_i, PACK]
+        def add_sums(engine, rel0, a_part, first_j, slots=slice(0, MAX_CHUNK), items=slice(0, BATCH), values=slice(0, NODES)):
+            shape = [P, slots.stop - slots.start, items.stop - items.start, values.stop - values.start, PACK]
             engine.tensor_tensor(
-                out=rel0[:, 0:size, :, :].rearrange("p j (b i) t -> p j b i t", b=BATCH)[:, :, :, first_i:last_i, :],
-                in0=a_part.rearrange("p (b i) t -> p b i t", b=BATCH)[:, :, first_i:last_i, :]
-                .unsqueeze(1)
-                .to_broadcast(shape),
-                in1=b_plus[:, first_j : first_j + size, :, :].unsqueeze(3).to_broadcast(shape),
-                op=ADD,
-            )
-
-        def add_item(engine, rel0, a_part, first_j, size, b, first_i):
-            shape = [P, size, NODES - first_i, PACK]
-            tokens = slice(b * NODES + first_i, (b + 1) * NODES)
-            engine.tensor_tensor(
-                out=rel0[:, 0:size, tokens, :],
-                in0=a_part[:, tokens, :].unsqueeze(1).to_broadcast(shape),
-                in1=b_plus[:, first_j : first_j + size, b, :].unsqueeze(2).to_broadcast(shape),
+                out=rel0[:, slots, :, :].rearrange("p j (b i) t -> p j b i t", b=BATCH)[:, :, items, values, :],
+                in0=a_part.rearrange("p (b i) t -> p b i t", b=BATCH)[:, items, values, :].unsqueeze(1).to_broadcast(shape),
+                in1=b_plus[:, first_j + slots.start : first_j + slots.stop, items, :].unsqueeze(3).to_broadcast(shape),
                 op=ADD,
             )
 
         def form_rel0(chunk):
-            first_j, size = starts[chunk], CHUNKS[chunk]
+            first_j = starts[chunk]
             rel0 = stream.tile([P, MAX_CHUNK, TOKENS, PACK], BF16, align_bytes=64)
-            cut = GP[chunk]
-            add_pairs(nc.gpsimd, rel0, a_sb[:], first_j, size, 0, cut)
-            for b in range(BATCH):
-                add_item(nc.vector, rel0, a_view, first_j, size, b, cut)
+            if chunk == 0 or chunk - 1 in FLIPPED:
+                cut = 1 if chunk == 0 else 2
+                add_sums(nc.gpsimd, rel0, a_sb[:], first_j, slots=slice(0, cut))
+                add_sums(nc.vector, rel0, a_view, first_j, slots=slice(cut, MAX_CHUNK))
+            else:
+                add_sums(nc.gpsimd, rel0, a_sb[:], first_j, values=slice(0, GPSIMD_I))
+                for b in range(BATCH):
+                    add_sums(nc.vector, rel0, a_view, first_j, items=slice(b, b + 1), values=slice(GPSIMD_I, NODES))
             return rel0
 
         def quantise_rel0(rel0, first_j, first_slot, last_slot):
@@ -365,6 +350,14 @@ def tile_languagemsgencoder_pa_kernel(
 
         rel0 = form_rel0(0)
         regroup(nc.vector.tensor_copy, ga_grouped, ga_raw, GA_CUT, F)
+        nc.vector.tensor_copy(
+            out=x2_codes[:].bitcast(I32).rearrange("p (e r) -> p e r", e=2),
+            in_=x_codes[:].bitcast(I32).unsqueeze(1).to_broadcast([P, 2, TOKENS]),
+        )
+        nc.vector.tensor_copy(
+            out=x2_scales[:].bitcast(I32).rearrange("p (e r) -> p e r", e=2),
+            in_=x_scales[:].bitcast(I32).unsqueeze(1).to_broadcast([P, 2, TOKENS // BYTES_PER_WORD]),
+        )
         ga = quantise_weight(nc, keep, ga_grouped, "ga")
         c_flipped = keep.tile([P, F // P, TOKENS], F32)
         (c_bank,) = flip_products([(ga, x_mx)], TOKENS)

from contextlib import ExitStack

import concourse.mybir as mybir
from concourse.masks import make_identity

BF16 = mybir.dt.bfloat16
F32 = mybir.dt.float32
I32 = mybir.dt.int32
U32 = mybir.dt.uint32
U8 = mybir.dt.uint8
FP8X4 = mybir.dt.float8_e4m3fn_x4
ADD = mybir.AluOpType.add
TANH = mybir.ActivationFunctionType.Tanh
IDENTITY = mybir.ActivationFunctionType.Identity

P = 128
PACK = 4
BATCH = 4
NODES = 32
TOKENS = BATCH * NODES
D = P * PACK
F = 512
PAIRS = BATCH * NODES * NODES

HALF = F // 2
HALVES = (slice(0, HALF), slice(HALF, F))

BYTES_PER_WORD = 4
WORDS = NODES // BYTES_PER_WORD
CHUNKS = [4] * 8
MAX_CHUNK = max(CHUNKS)
GA_CUT = F - P // 2
M_CUT = P // 2
GC_CUT = 3 * P
WARM_UP_PASSES = 12
NEW_X_CHUNK = 5
GO_CHUNK = 3
FLIPPED = (0, 2, 4)
ACC_BANKS = 3
GPSIMD_I = 20


FLOPS = 2 * (5 * TOKENS * D * F + PAIRS * D * F)


def load_weight(nc, pool, rows, name):
    raw = pool.tile([P, PACK, F], BF16, name=name)
    nc.sync.dma_start(out=raw[:], in_=rows.rearrange("(p t) n -> p t n", p=P))
    return raw


def new_grouped(pool, name):
    return pool.tile([P, F, PACK], BF16, name=name, align_bytes=64)


def regroup(copy, grouped, raw, first=0, last=F):
    copy(
        out=grouped[:, first:last, :].rearrange("p (c i) t -> p c t i", i=4),
        in_=raw[:, :, first:last].rearrange("p t (c i) -> p c t i", i=4),
    )


def regroup_by_channel(copy, grouped, raw, first, last):
    copy(
        out=grouped[:].rearrange("p (t m) j -> p m j t", t=PACK)[:, first:last, :, :],
        in_=raw[:].rearrange("p j (m t) -> p m j t", t=PACK)[:, first:last, :, :],
    )


def quantise_weight(nc, pool, grouped, name):
    codes = pool.tile([P, F], U32, name=name + "_codes", align_bytes=64)
    scales = pool.tile([P, F], U8, name=name + "_scales", align_bytes=64)
    nc.vector.quantize_mx(
        out=codes[:].bitcast(FP8X4), scales=scales[:], in_=grouped[:].rearrange("p n t -> p (n t)")
    )
    return codes, scales


def columns(operand, first, count):
    codes, scales = operand
    return codes[:, first : first + count], scales[:, first : first + count]


def mx_pass(nc, out, stationary, moving, start, stop):
    nc.tensor.matmul_mx(
        out=out,
        lhsT=stationary[0].bitcast(FP8X4),
        lhsT_scale=stationary[1],
        rhs=moving[0].bitcast(FP8X4),
        rhs_scale=moving[1],
        start=start,
        stop=stop,
    )


def tile_languagemsgencoder_pa_kernel(
    tc, text_embedding, W_rel, b_rel, W_go, b_go, W_gr, b_gr, out_0, out_1
):
    nc = tc.nc
    new_x_rows = out_0.rearrange("b n f -> (b n) f")
    rel_rows = out_1.rearrange("b i j f -> (b i) j f")

    with ExitStack() as ctx:
        keep = ctx.enter_context(tc.tile_pool(name="keep", bufs=1))
        stream = ctx.enter_context(tc.tile_pool(name="stream", bufs=1))
        results = ctx.enter_context(tc.tile_pool(name="results", bufs=8))
        flips = ctx.enter_context(tc.tile_pool(name="flips", bufs=2))
        keep_ps = ctx.enter_context(tc.psum_pool(name="keep_ps", bufs=1))
        setup_ps = ctx.enter_context(tc.psum_pool(name="setup_ps", bufs=4))
        acc_ps = ctx.enter_context(tc.psum_pool(name="acc_ps", bufs=ACC_BANKS))
        ctx.enter_context(tc.manual_schedule())

        warm = keep.tile([P, 1], F32)
        nc.vector.memset(warm[:], 0.0)
        nc.scalar.activation(out=warm[:], in_=warm[:], func=TANH)

        ident = keep.tile([P, P], F32)
        make_identity(nc, ident[:])

        bias_rows = keep.tile([P, 3, F], BF16)
        nc.vector.memset(bias_rows[:].rearrange("p a f -> p (a f)").bitcast(I32), 0)
        ones = keep.tile([P, P], BF16)
        nc.vector.memset(ones[:], 1.0)

        x_sb = keep.tile([P, D], BF16)
        nc.sync.dma_start(out=x_sb[:], in_=text_embedding.rearrange("b n d -> (b n) d"))
        rb_raw = load_weight(nc, keep, W_rel[D : 2 * D, :], "rb_raw")
        for row, bias in enumerate((b_rel, b_gr, b_go)):
            nc.sync.dma_start(out=bias_rows[0:1, row, :], in_=bias.rearrange("(o f) -> o f", o=1))
        ra_raw = load_weight(nc, keep, W_rel[0:D, :], "ra_raw")
        gc_raw = load_weight(nc, keep, W_gr[2 * D : 3 * D, :], "gc_raw")
        gb_raw = load_weight(nc, keep, W_gr[D : 2 * D, :], "gb_raw")
        ga_raw = load_weight(nc, keep, W_gr[0:D, :], "ga_raw")
        go_raw = load_weight(nc, keep, W_go, "go_raw")

        x_codes = keep.tile([P, TOKENS], U32, align_bytes=64)
        x_scales = keep.tile([P, TOKENS], U8, align_bytes=64)
        nc.vector.memset(x_scales[:].bitcast(I32), 0)

        x_words = x_sb[:].bitcast(F32)
        x_t = setup_ps.tile([P, 2, TOKENS], F32, tag="setup")
        for u in range(2):
            nc.tensor.transpose(x_t[:, u, :], x_words[:, u : D // 2 : 2], ident[:])
        rb_grouped = new_grouped(keep, "rb_grouped")
        ra_grouped = new_grouped(keep, "ra_grouped")
        x_grouped = keep.tile([P, TOKENS, PACK], BF16, align_bytes=64)
        nc.scalar.copy(
            out=x_grouped[:].rearrange("p r t -> p (r t)").bitcast(F32).rearrange("p (r u) -> p r u", u=2),
            in_=x_t[:].rearrange("p u r -> p r u"),
        )
        bias_t = setup_ps.tile([P, 3, PACK], F32, tag="setup")
        for t in range(PACK):
            for row, values in enumerate((slice(t, F, PACK), slice(t * P, (t + 1) * P), slice(t * P, (t + 1) * P))):
                nc.tensor.matmul(
                    out=bias_t[:, row, t : t + 1], lhsT=bias_rows[:, row, values], rhs=ones[:, 0:1], start=True, stop=True
                )
        bias_cols = keep.tile([P, 3, PACK], F32)
        brel = bias_cols[:, 0, :]
        bgr_cols = bias_cols[:, 1, :]
        bgo_cols = bias_cols[:, 2, :]
        nc.vector.quantize_mx(
            out=x_codes[:].bitcast(FP8X4), scales=x_scales[:], in_=x_grouped[:].rearrange("p r t -> p (r t)")
        )
        x_mx = (x_codes[:], x_scales[:])
        x4_scales = keep.tile([P, TOKENS, BYTES_PER_WORD], U8, align_bytes=64)
        for c in range(BYTES_PER_WORD):
            nc.vector.tensor_copy(out=x4_scales[:, :, c], in_=x_scales[:])
        x4_words = x4_scales[:].rearrange("p r c -> p (r c)").bitcast(I32)

        regroup_by_channel(nc.vector.tensor_copy, rb_grouped, rb_raw, 0, M_CUT)
        regroup_by_channel(nc.scalar.copy, rb_grouped, rb_raw, M_CUT, P)
        nc.vector.tensor_copy(out=bias_cols[:], in_=bias_t[:])
        x2_codes = keep.tile([P, 2 * TOKENS], U32, align_bytes=64)
        x2_scales = keep.tile([P, 2 * TOKENS], U8, align_bytes=64)

        rel0_codes = keep.tile([P, PAIRS], U32, align_bytes=64)
        rel0_scales = keep.tile([P, PAIRS], U8, align_bytes=64)
        rel0_mx = (rel0_codes, rel0_scales)
        xj_codes = keep.tile([P, PAIRS], U32, align_bytes=64)
        xj_scales = keep.tile([P, PAIRS], U8, align_bytes=64)
        xj = (xj_codes, xj_scales)

        def repeat_xj(first_j, last_j):
            count = last_j - first_j
            nc.vector.tensor_copy(
                out=xj_codes[:].bitcast(I32).rearrange("p (j b i) -> p j b i", b=BATCH, i=NODES)[:, first_j:last_j, :, :],
                in_=x_codes[:]
                .bitcast(I32)
                .rearrange("p (b j) -> p j b", b=BATCH)[:, first_j:last_j, :]
                .unsqueeze(3)
                .to_broadcast([P, count, BATCH, NODES]),
            )
            nc.vector.tensor_copy(
                out=xj_scales[:].bitcast(I32).rearrange("p (j b w) -> p j b w", b=BATCH, w=WORDS)[:, first_j:last_j, :, :],
                in_=x4_words.rearrange("p (b j) -> p j b", b=BATCH)[:, first_j:last_j, :]
                .unsqueeze(3)
                .to_broadcast([P, count, BATCH, WORDS]),
            )

        def warm_up(count):
            idle = setup_ps.tile([P, F], F32, tag="setup")
            for n in range(count):
                mx_pass(nc, idle[:], x_mx, columns(rb, 0, F), start=True, stop=True)

        rb = quantise_weight(nc, keep, rb_grouped, "rb")
        b_t = setup_ps.tile([P, PACK, TOKENS], F32, tag="setup")
        for t in range(PACK):
            mx_pass(nc, b_t[:, t, :], columns(rb, t * P, P), x_mx, start=True, stop=True)
        regroup_by_channel(nc.vector.tensor_copy, ra_grouped, ra_raw, 0, M_CUT)
        regroup_by_channel(nc.scalar.copy, ra_grouped, ra_raw, M_CUT, P)
        ra = quantise_weight(nc, keep, ra_grouped, "ra")
        gc_grouped = new_grouped(keep, "gc_grouped")
        gb_grouped = new_grouped(keep, "gb_grouped")
        ga_grouped = new_grouped(keep, "ga_grouped")
        go_grouped = new_grouped(keep, "go_grouped")
        b_plus = keep.tile([P, NODES, BATCH, PACK], F32)
        nc.vector.tensor_tensor(
            out=b_plus[:].rearrange("p j b t -> p b j t"),
            in0=b_t[:].rearrange("p t (b j) -> p b j t", b=BATCH),
            in1=brel.unsqueeze(1).unsqueeze(1).to_broadcast([P, BATCH, NODES, PACK]),
            op=ADD,
        )
        regroup(nc.scalar.copy, gc_grouped, gc_raw, 0, GC_CUT)
        starts = [sum(CHUNKS[:c]) for c in range(len(CHUNKS))]
        repeat_xj(0, starts[2])
        regroup(nc.vector.tensor_copy, gb_grouped, gb_raw)
        a_t = keep_ps.tile([P, PACK, TOKENS], F32)
        for t in range(PACK):
            mx_pass(nc, a_t[:, t, :], columns(ra, t * P, P), x_mx, start=True, stop=True)
        warm_up(WARM_UP_PASSES)
        a_sb = keep.tile([P, TOKENS, PACK], F32)
        nc.scalar.copy(out=a_sb[:], in_=a_t[:].rearrange("p t r -> p r t"))
        regroup(nc.scalar.copy, gc_grouped, gc_raw, GC_CUT, F)
        regroup(nc.scalar.copy, ga_grouped, ga_raw, 0, GA_CUT)

        a_view = a_t[:].rearrange("p t r -> p r t")

        def add_sums(engine, rel0, a_part, first_j, slots=slice(0, MAX_CHUNK), items=slice(0, BATCH), values=slice(0, NODES)):
            shape = [P, slots.stop - slots.start, items.stop - items.start, values.stop - values.start, PACK]
            engine.tensor_tensor(
                out=rel0[:, slots, :, :].rearrange("p j (b i) t -> p j b i t", b=BATCH)[:, :, items, values, :],
                in0=a_part.rearrange("p (b i) t -> p b i t", b=BATCH)[:, items, values, :].unsqueeze(1).to_broadcast(shape),
                in1=b_plus[:, first_j + slots.start : first_j + slots.stop, items, :].unsqueeze(3).to_broadcast(shape),
                op=ADD,
            )

        def form_rel0(chunk):
            first_j = starts[chunk]
            rel0 = stream.tile([P, MAX_CHUNK, TOKENS, PACK], BF16, align_bytes=64)
            if chunk == 0 or chunk - 1 in FLIPPED:
                cut = 1 if chunk == 0 else 2
                add_sums(nc.gpsimd, rel0, a_sb[:], first_j, slots=slice(0, cut))
                add_sums(nc.vector, rel0, a_view, first_j, slots=slice(cut, MAX_CHUNK))
            else:
                add_sums(nc.gpsimd, rel0, a_sb[:], first_j, values=slice(0, GPSIMD_I))
                for b in range(BATCH):
                    add_sums(nc.vector, rel0, a_view, first_j, items=slice(b, b + 1), values=slice(GPSIMD_I, NODES))
            return rel0

        def quantise_rel0(rel0, first_j, first_slot, last_slot):
            codes, scales = columns(rel0_mx, (first_j + first_slot) * TOKENS, (last_slot - first_slot) * TOKENS)
            nc.vector.quantize_mx(
                out=codes.bitcast(FP8X4),
                scales=scales,
                in_=rel0[:, first_slot:last_slot, :, :].rearrange("p s r t -> p (s r t)"),
            )

        def open_tile(j):
            acc = acc_ps.tile([P, F], F32, tag="acc")
            mx_pass(nc, acc[:], columns(xj, j * TOKENS, TOKENS), columns(gb, 0, F), start=True, stop=False)
            return acc

        def close_tile(acc, j):
            mx_pass(nc, acc[:], columns(rel0_mx, j * TOKENS, TOKENS), columns(gc, 0, F), start=False, stop=True)

        def finish(acc, addend, result):
            nc.vector.tensor_tensor(out=result, in0=acc, in1=addend, op=ADD)
            nc.scalar.activation(out=result, in_=result, func=TANH)

        def flip_products(terms, width):
            blocks = F // width
            banks = []
            for block in range(F // P):
                if block % blocks == 0:
                    bank = setup_ps.tile([P, blocks, width], F32, tag="setup")
                    banks.append(bank)
                for n, (weight, moving) in enumerate(terms):
                    mx_pass(
                        nc,
                        banks[-1][:, block % blocks, :],
                        columns(weight, block * P, P),
                        moving,
                        start=n == 0,
                        stop=n == len(terms) - 1,
                    )
            return banks

        def flip_out(bank, first, flipped, func, bias_cols):
            for u in range(bank.shape[1]):
                block = first + u
                nc.scalar.activation(
                    out=flipped[:, block, :], in_=bank[:, u, :], func=func, bias=bias_cols[:, block : block + 1]
                )

        def flip_back(flipped, slot):
            bank = setup_ps.tile([P, F], F32, tag="setup")
            for block in range(F // P):
                nc.tensor.transpose(
                    bank[:, block * P : (block + 1) * P], flipped[:, block, slot * TOKENS : (slot + 1) * TOKENS], ident[:]
                )
            return bank

        def flip_of(chunk):
            if chunk in FLIPPED:
                j = starts[chunk] + CHUNKS[chunk] - 2
                x2 = (x2_codes[:], x2_scales[:])
                terms = [(gb, columns(xj, j * TOKENS, 2 * TOKENS)), (ga, x2), (gc, columns(rel0_mx, j * TOKENS, 2 * TOKENS))]
                return terms, 2, bgr_cols, [rel_rows[:, j, :], rel_rows[:, j + 1, :]]
            if chunk == NEW_X_CHUNK:
                return [(go, x_mx)], 1, bgo_cols, [new_x_rows]
            return None

        def straight_tiles(chunk):
            first, size = starts[chunk], CHUNKS[chunk]
            return list(range(first, first + (size - 2 if chunk in FLIPPED else size)))

        to_open = [j for chunk in range(len(CHUNKS)) for j in straight_tiles(chunk)]
        accs = {}
        in_banks = []
        quantised = [0]

        def open_tiles(limit):
            while to_open and to_open[0] < limit and len(in_banks) < ACC_BANKS:
                j = to_open[0]
                to_open.remove(j)
                in_banks.append(j)
                accs[j] = open_tile(j)
                if j < quantised[0]:
                    close_tile(accs[j], j)

        def quantise_chunk(rel0, chunk):
            first, size = starts[chunk], CHUNKS[chunk]
            step = size // 2 if chunk == len(CHUNKS) - 1 else size
            for slot in range(0, size, step):
                quantise_rel0(rel0, first, slot, slot + step)
                quantised[0] = first + slot + step
                for j in straight_tiles(chunk):
                    if j in accs and first + slot <= j < quantised[0]:
                        close_tile(accs[j], j)

        rel0 = form_rel0(0)
        regroup(nc.vector.tensor_copy, ga_grouped, ga_raw, GA_CUT, F)
        nc.vector.tensor_copy(
            out=x2_codes[:].bitcast(I32).rearrange("p (e r) -> p e r", e=2),
            in_=x_codes[:].bitcast(I32).unsqueeze(1).to_broadcast([P, 2, TOKENS]),
        )
        nc.vector.tensor_copy(
            out=x2_scales[:].bitcast(I32).rearrange("p (e r) -> p e r", e=2),
            in_=x_scales[:].bitcast(I32).unsqueeze(1).to_broadcast([P, 2, TOKENS // BYTES_PER_WORD]),
        )
        ga = quantise_weight(nc, keep, ga_grouped, "ga")
        c_flipped = keep.tile([P, F // P, TOKENS], F32)
        (c_bank,) = flip_products([(ga, x_mx)], TOKENS)
        regroup(nc.scalar.copy, go_grouped, go_raw, 0, HALF)
        flip_out(c_bank, 0, c_flipped[:], IDENTITY, bgr_cols)
        gb = quantise_weight(nc, keep, gb_grouped, "gb")
        open_tiles(starts[2])
        c_back = flip_back(c_flipped[:], 0)
        c_gr = keep.tile([P, F], F32)
        nc.scalar.copy(out=c_gr[:], in_=c_back[:])
        gc = quantise_weight(nc, keep, gc_grouped, "gc")
        quantise_chunk(rel0, 0)

        flipped = None
        last = len(CHUNKS)
        for chunk in range(1, last + 2):
            backs = []
            if flipped:
                backs = [flip_back(flipped, slot) for slot in range(back_tiles)]
                back_rows = flip_rows
            flip = flip_of(chunk - 1)
            flipped = None
            if flip:
                terms, back_tiles, bias, flip_rows = flip
                products = flip_products(terms, back_tiles * TOKENS)
            if chunk < last:
                rel0 = form_rel0(chunk)
            if backs:
                result = results.tile([P, 2, F], F32, name="result")
                for slot, back in enumerate(backs):
                    nc.scalar.copy(out=result[:, slot, :], in_=back[:])
                    nc.sync.dma_start(out=back_rows[slot], in_=result[:, slot, :])
            straight = straight_tiles(chunk - 1) if chunk <= last else []
            if flip:
                flipped = flips.tile([P, F // P, 2 * TOKENS], F32, name="flipped")
                flipped = flipped[:, :, 0 : back_tiles * TOKENS]
            for n in range(max(len(straight), 2)):
                if flip and n < len(products):
                    flip_out(products[n], n * (F // P) // len(products), flipped, TANH, bias)
                if n < len(straight):
                    j = straight[n]
                    if n % 2 == 0:
                        result = results.tile([P, 2, F], F32, name="result")
                    for part in HALVES if chunk == last else (slice(0, F),):
                        finish(accs[j][:, part], c_gr[:, part], result[:, n % 2, part])
                    in_banks.remove(j)
                    open_tiles(starts[chunk + 1] if chunk + 1 < last else NODES)
                    if chunk >= last - 1:
                        nc.sync.dma_start(out=rel_rows[:, j, :], in_=result[:, n % 2, :])
                    elif n % 2 == 1:
                        nc.sync.dma_start(out=rel_rows[:, j - 1 : j + 1, :], in_=result[:])
            if chunk < last:
                quantise_chunk(rel0, chunk)
            if chunk + 1 < last:
                repeat_xj(starts[chunk + 1], starts[chunk + 1] + CHUNKS[chunk + 1])
            if chunk == GO_CHUNK:
                regroup(nc.scalar.copy, go_grouped, go_raw, HALF, F)
            if chunk == NEW_X_CHUNK:
                go = quantise_weight(nc, keep, go_grouped, "go")
